import numpy as np
import ml_dtypes


def mxq(x, axis, fmt="e4m3"):
    dtype, down = {"e4m3": (ml_dtypes.float8_e4m3fn, 7), "e5m2": (ml_dtypes.float8_e5m2, 14)}[fmt]
    v = np.moveaxis(np.asarray(x, np.float32).astype(ml_dtypes.bfloat16).astype(np.float64), axis, -1)
    blocks = v.reshape(v.shape[:-1] + (-1, 32))
    amax = np.abs(blocks).max(-1, keepdims=True)
    byte = np.maximum(np.where(amax > 0, np.frexp(amax)[1] - 1 + 127, 0) - down, 1)
    scale = np.exp2(byte - 127.0)
    codes = (blocks / scale).astype(np.float32).astype(dtype).astype(np.float64)
    return np.moveaxis((codes * scale).reshape(v.shape), -1, axis)


WIDE = False


def mx_kscale(k):
    if not WIDE:
        return np.ones(k)
    levels = np.array([10, -10, 5, -5, 0])
    a = np.random.permutation(np.resize(levels, k // 512 * 4)).reshape(k // 512, 4)
    idx = np.arange(k)
    return np.exp2(a[idx // 512, idx % 128 // 32])


BF16 = ml_dtypes.bfloat16


def bf(x):
    return np.asarray(x, np.float32).astype(BF16)


def f64(x):
    return np.asarray(x).astype(np.float64)


N, D_IN, UNITS = 4096, 512, 512


def setup_inputs():
    s = mx_kscale(D_IN)
    cu, cw = 0.6 / np.sqrt(D_IN), 0.6 / np.sqrt(UNITS)
    return {"X": bf(np.random.standard_normal((N, D_IN)) * s),
            "S": bf(np.random.standard_normal((N, UNITS))),
            "H": bf(np.tanh(np.random.standard_normal((N, UNITS)) * 0.8)),
            "Uz": bf(np.random.standard_normal((D_IN, UNITS)) * cu / s[:, None]),
            "Ug": bf(np.random.standard_normal((D_IN, UNITS)) * cu / s[:, None]),
            "Wz": bf(np.random.standard_normal((UNITS, UNITS)) * cw),
            "Wg": bf(np.random.standard_normal((UNITS, UNITS)) * cw),
            "bz": bf(np.random.standard_normal(UNITS) * 0.3),
            "bg": bf(np.random.standard_normal(UNITS) * 0.3)}


def reference(X, S, H, Uz, Ug, Wz, Wg, bz, bg):
    xq = mxq(f64(X), 1, "e4m3")
    Sf = f64(S)
    sq = mxq(Sf, 1, "e4m3")
    Z = np.tanh((xq @ mxq(f64(Uz), 0, "e4m3")) + (sq @ mxq(f64(Wz), 0, "e4m3")) + f64(bz))
    G = np.tanh((xq @ mxq(f64(Ug), 0, "e4m3")) + (sq @ mxq(f64(Wg), 0, "e4m3")) + f64(bg))
    return (1.0 - G) * f64(H) + Z * Sf

@@ -1,0 +1,236 @@
+from contextlib import ExitStack
+
+import concourse.mybir as mybir
+from concourse.masks import make_identity
+
+F32 = mybir.dt.float32
+BF16 = mybir.dt.bfloat16
+U32 = mybir.dt.uint32
+U8 = mybir.dt.uint8
+FP8X4 = mybir.dt.float8_e4m3fn_x4
+ALU = mybir.AluOpType
+TANH = mybir.ActivationFunctionType.Tanh
+
+P = 128
+ROWS = 4096
+FEATURES = 512
+PACK = 4
+HALVES = 2
+WORDS = FEATURES // 2
+BLOCK_ROWS = 512
+ROW_TILES = BLOCK_ROWS // P
+BLOCKS = ROWS // BLOCK_ROWS
+UNIT_CHUNKS = FEATURES // P
+GATE_Z = 0
+GATE_G = 1
+GATES = 2
+STEPS = BLOCKS * GATES
+OPERANDS = BLOCKS * 2
+TRANSPOSE_LEAD = 3
+LOAD_LEAD = 3
+
+FLOPS = 4 * 2 * ROWS * FEATURES * FEATURES
+
+
+def tile_lstmlayer_pb_t_kernel(tc, X, S, H, Uz, Ug, Wz, Wg, bz, bg, out):
+    nc = tc.nc
+
+    def blocks_of(dram):
+        return dram.rearrange("(b p j) d -> b p (j d)", p=P, j=ROW_TILES)
+
+    x_blocks, s_blocks, h_blocks, out_blocks = blocks_of(X), blocks_of(S), blocks_of(H), blocks_of(out)
+
+    with ExitStack() as ctx:
+        consts = ctx.enter_context(tc.tile_pool(name="consts", bufs=1))
+        inputs = ctx.enter_context(tc.tile_pool(name="inputs", bufs=BLOCKS))
+        regroup = ctx.enter_context(tc.tile_pool(name="regroup", bufs=2))
+        quantised = ctx.enter_context(tc.tile_pool(name="quantised", bufs=4))
+        gates = ctx.enter_context(tc.tile_pool(name="gates", bufs=3))
+        mixes = ctx.enter_context(tc.tile_pool(name="mixes", bufs=2))
+        mx_psum = ctx.enter_context(tc.psum_pool(name="mx_psum", bufs=4))
+        tp_psum = ctx.enter_context(tc.psum_pool(name="tp_psum", bufs=4))
+        ctx.enter_context(tc.manual_schedule())
+
+        x_sb, s_sb, h_sb = {}, {}, {}
+
+        def load(dram_block, name):
+            tile_sb = inputs.tile([P, ROW_TILES * FEATURES], BF16, name=name)
+            nc.sync.dma_start(out=tile_sb[:], in_=dram_block)
+            return tile_sb
+
+        def load_x_and_s(b):
+            x_sb[b] = load(x_blocks[b], "x_sb")
+            s_sb[b] = load(s_blocks[b], "s_sb")
+
+        def load_weight(w, name):
+            raw = consts.tile([P, PACK, FEATURES], BF16, name=name)
+            nc.sync.dma_start(
+                out=raw[:].rearrange("p (u e) n -> p u e n", e=2),
+                in_=w.rearrange("(u p e) n -> p u e n", u=HALVES, e=2),
+            )
+            return raw
+
+        def regroup_weight(raw):
+            grouped = regroup.tile([P, FEATURES, PACK], BF16, name="w_grouped", align_bytes=64)
+            nc.vector.tensor_copy(out=grouped[:], in_=raw[:].rearrange("p t n -> p n t"))
+            return grouped
+
+        def quantise(grouped_flat, pool, name):
+            codes = pool.tile([P, FEATURES], U32, name=name + "_codes", align_bytes=64)
+            scales = pool.tile([P, FEATURES], U8, name=name + "_scales", align_bytes=64)
+            nc.vector.quantize_mx(out=codes[:].bitcast(FP8X4), scales=scales[:], in_=grouped_flat)
+            return codes, scales
+
+        def quantise_gate_weights(raw_u, raw_w, name):
+            grouped_u = regroup_weight(raw_u)
+            grouped_w = regroup_weight(raw_w)
+            return [
+                quantise(grouped_u[:].rearrange("p n t -> p (n t)"), consts, "u" + name),
+                quantise(grouped_w[:].rearrange("p n t -> p (n t)"), consts, "w" + name),
+            ]
+
+        ident = consts.tile([P, P], F32, name="ident")
+        make_identity(nc, ident[:])
+
+        warm = consts.tile([P, 2], F32, name="warm")
+        nc.vector.memset(warm[:], 0.0)
+        nc.scalar.activation(out=warm[:, 1:2], in_=warm[:, 0:1], func=TANH)
+
+        bias_rows = consts.tile([P, P], BF16, name="bias_rows")
+        nc.vector.memset(bias_rows[:], 0.0)
+        for gate, bias in ((GATE_Z, bz), (GATE_G, bg)):
+            nc.sync.dma_start(
+                out=bias_rows[gate * UNIT_CHUNKS : (gate + 1) * UNIT_CHUNKS, :],
+                in_=bias.rearrange("(c m) -> c m", m=P),
+            )
+
+        raw_uz = load_weight(Uz, "raw_uz")
+        x_sb[0] = load(x_blocks[0], "x_sb")
+        raw_wz = load_weight(Wz, "raw_wz")
+        s_sb[0] = load(s_blocks[0], "s_sb")
+        raw_ug = load_weight(Ug, "raw_ug")
+        raw_wg = load_weight(Wg, "raw_wg")
+        for b in range(1, LOAD_LEAD):
+            load_x_and_s(b)
+            h_sb[b - 1] = load(h_blocks[b - 1], "h_sb")
+
+        bias_rows_f32 = consts.tile([P, P], F32, name="bias_rows_f32")
+        nc.vector.tensor_copy(out=bias_rows_f32[:], in_=bias_rows[:])
+        bias_bank = tp_psum.tile([P, P], F32, name="bias_bank", tag="tp")
+        nc.tensor.transpose(out=bias_bank[:], in_=bias_rows_f32[:], identity=ident[:])
+        bias_col = consts.tile([P, GATES * UNIT_CHUNKS], F32, name="bias_col")
+        nc.vector.tensor_copy(out=bias_col[:], in_=bias_bank[:, 0 : GATES * UNIT_CHUNKS])
+
+        grouped_of = {}
+        operand_q = {}
+        weight_q = {}
+        tanh_of = {}
+        zs_sb, gh_sb = {}, {}
+
+        def transpose_operand(q):
+            source = x_sb[q // 2] if q % 2 == 0 else s_sb[q // 2]
+            words = source[:].bitcast(F32)
+            grouped = regroup.tile([P, BLOCK_ROWS * PACK], BF16, name="a_grouped", align_bytes=64)
+            grouped_words = grouped[:].bitcast(F32)
+            for pair in range(ROW_TILES // 2):
+                bank = tp_psum.tile([P, 2, HALVES, P], F32, name="in_bank", tag="tp")
+                for i in range(2):
+                    first = (2 * pair + i) * WORDS
+                    for u in range(HALVES):
+                        nc.tensor.transpose(
+                            out=bank[:, i, u, :],
+                            in_=words[:, first + u * P : first + (u + 1) * P],
+                            identity=ident[:],
+                        )
+                nc.scalar.copy(
+                    out=grouped_words[:, pair * 2 * WORDS : (pair + 1) * 2 * WORDS].rearrange(
+                        "p (i r u) -> p i r u", i=2, u=HALVES
+                    ),
+                    in_=bank[:].rearrange("p i u r -> p i r u"),
+                )
+            grouped_of[q] = grouped
+
+        def quantise_operand(q):
+            operand_q[q] = quantise(grouped_of[q][:], quantised, "a")
+
+        def gate_matmuls(step):
+            b, gate = divmod(step, GATES)
+            result = gates.tile([P, UNIT_CHUNKS, BLOCK_ROWS], F32, name="tanh_sb")
+            for c in range(UNIT_CHUNKS):
+                units = slice(c * P, (c + 1) * P)
+                acc = mx_psum.tile([P, BLOCK_ROWS], F32, name="acc")
+                for side in range(2):
+                    w_codes, w_scales = weight_q[gate][side]
+                    a_codes, a_scales = operand_q[2 * b + side]
+                    nc.tensor.matmul_mx(
+                        out=acc[:],
+                        lhsT=w_codes[:, units].bitcast(FP8X4),
+                        lhsT_scale=w_scales[:, units],
+                        rhs=a_codes[:].bitcast(FP8X4),
+                        rhs_scale=a_scales[:],
+                        start=(side == 0),
+                        stop=(side == 1),
+                    )
+                column = gate * UNIT_CHUNKS + c
+                nc.scalar.activation(
+                    out=result[:, c, :], in_=acc[:], func=TANH, bias=bias_col[:, column : column + 1], scale=1.0
+                )
+            tanh_of[step] = result
+
+        def mix(step):
+            b, gate = divmod(step, GATES)
+            if gate == GATE_Z:
+                zs_sb[b] = mixes.tile([P, ROW_TILES * FEATURES], F32, name="zs_sb")
+            else:
+                gh_sb[b] = mixes.tile([P, ROW_TILES * FEATURES], F32, name="gh_sb")
+            for j in range(ROW_TILES):
+                bank = tp_psum.tile([P, FEATURES], F32, name="back_bank", tag="tp")
+                for c in range(UNIT_CHUNKS):
+                    nc.tensor.transpose(
+                        out=bank[:, c * P : (c + 1) * P],
+                        in_=tanh_of[step][:, c, j * P : (j + 1) * P],
+                        identity=ident[:],
+                    )
+                cols = slice(j * FEATURES, (j + 1) * FEATURES)
+                if gate == GATE_Z:
+                    nc.vector.tensor_tensor(out=zs_sb[b][:, cols], in0=bank[:], in1=s_sb[b][:, cols], op=ALU.mult)
+                else:
+                    nc.vector.scalar_tensor_tensor(
+                        out=gh_sb[b][:, cols],
+                        in0=bank[:],
+                        scalar=1.0,
+                        in1=h_sb[b][:, cols],
+                        op0=ALU.subtract,
+                        op1=ALU.mult,
+                    )
+                    nc.gpsimd.tensor_tensor(
+                        out=zs_sb[b][:, cols], in0=zs_sb[b][:, cols], in1=gh_sb[b][:, cols], op=ALU.subtract
+                    )
+            if gate == GATE_G:
+                nc.sync.dma_start(out=out_blocks[b], in_=zs_sb[b][:])
+
+        weight_q[GATE_Z] = quantise_gate_weights(raw_uz, raw_wz, "z")
+        transpose_operand(0)
+        transpose_operand(1)
+        quantise_operand(0)
+        quantise_operand(1)
+        weight_q[GATE_G] = quantise_gate_weights(raw_ug, raw_wg, "g")
+        transposed = 2
+
+        for step in range(STEPS):
+            b, gate = divmod(step, GATES)
+            if gate == GATE_Z:
+                if b + LOAD_LEAD < BLOCKS:
+                    load_x_and_s(b + LOAD_LEAD)
+                if b + LOAD_LEAD - 1 < BLOCKS:
+                    h_sb[b + LOAD_LEAD - 1] = load(h_blocks[b + LOAD_LEAD - 1], "h_sb")
+            gate_matmuls(step)
+            if step > 0:
+                mix(step - 1)
+            until = min(step + TRANSPOSE_LEAD + 1, OPERANDS)
+            for q in range(transposed, until):
+                transpose_operand(q)
+            for q in range(transposed, until):
+                quantise_operand(q)
+            transposed = until
+        mix(STEPS - 1)

@@ -28,6 +28,11 @@ STEPS = BLOCKS * GATES
 OPERANDS = BLOCKS * 2
 TRANSPOSE_LEAD = 3
 LOAD_LEAD = 3
+ROUNDS = 2
+CHUNKS_A_ROUND = UNIT_CHUNKS // ROUNDS
+ROW_TILES_A_ROUND = ROW_TILES // ROUNDS
+BANK_ROW_TILES = 2
+IN_BANKS_A_ROUND = ROW_TILES // BANK_ROW_TILES // ROUNDS
 
 FLOPS = 4 * 2 * ROWS * FEATURES * FEATURES
 
@@ -127,15 +132,16 @@ def tile_lstmlayer_pb_t_kernel(tc, X, S, H, Uz, Ug, Wz, Wg, bz, bg, out):
         tanh_of = {}
         zs_sb, gh_sb = {}, {}
 
-        def transpose_operand(q):
+        def transpose_operand(q, part):
             source = x_sb[q // 2] if q % 2 == 0 else s_sb[q // 2]
             words = source[:].bitcast(F32)
-            grouped = regroup.tile([P, BLOCK_ROWS * PACK], BF16, name="a_grouped", align_bytes=64)
-            grouped_words = grouped[:].bitcast(F32)
-            for pair in range(ROW_TILES // 2):
-                bank = tp_psum.tile([P, 2, HALVES, P], F32, name="in_bank", tag="tp")
-                for i in range(2):
-                    first = (2 * pair + i) * WORDS
+            if part == 0:
+                grouped_of[q] = regroup.tile([P, BLOCK_ROWS * PACK], BF16, name="a_grouped", align_bytes=64)
+            grouped_words = grouped_of[q][:].bitcast(F32)
+            for pair in range(part * IN_BANKS_A_ROUND, (part + 1) * IN_BANKS_A_ROUND):
+                bank = tp_psum.tile([P, BANK_ROW_TILES, HALVES, P], F32, name="in_bank", tag="tp")
+                for i in range(BANK_ROW_TILES):
+                    first = (BANK_ROW_TILES * pair + i) * WORDS
                     for u in range(HALVES):
                         nc.tensor.transpose(
                             out=bank[:, i, u, :],
@@ -143,20 +149,20 @@ def tile_lstmlayer_pb_t_kernel(tc, X, S, H, Uz, Ug, Wz, Wg, bz, bg, out):
                             identity=ident[:],
                         )
                 nc.scalar.copy(
-                    out=grouped_words[:, pair * 2 * WORDS : (pair + 1) * 2 * WORDS].rearrange(
-                        "p (i r u) -> p i r u", i=2, u=HALVES
+                    out=grouped_words[:, pair * BANK_ROW_TILES * WORDS : (pair + 1) * BANK_ROW_TILES * WORDS].rearrange(
+                        "p (i r u) -> p i r u", i=BANK_ROW_TILES, u=HALVES
                     ),
                     in_=bank[:].rearrange("p i u r -> p i r u"),
                 )
-            grouped_of[q] = grouped
 
         def quantise_operand(q):
             operand_q[q] = quantise(grouped_of[q][:], quantised, "a")
 
-        def gate_matmuls(step):
+        def gate_matmuls(step, part):
             b, gate = divmod(step, GATES)
-            result = gates.tile([P, UNIT_CHUNKS, BLOCK_ROWS], F32, name="tanh_sb")
-            for c in range(UNIT_CHUNKS):
+            if part == 0:
+                tanh_of[step] = gates.tile([P, UNIT_CHUNKS, BLOCK_ROWS], F32, name="tanh_sb")
+            for c in range(part * CHUNKS_A_ROUND, (part + 1) * CHUNKS_A_ROUND):
                 units = slice(c * P, (c + 1) * P)
                 acc = mx_psum.tile([P, BLOCK_ROWS], F32, name="acc")
                 for side in range(2):
@@ -173,17 +179,16 @@ def tile_lstmlayer_pb_t_kernel(tc, X, S, H, Uz, Ug, Wz, Wg, bz, bg, out):
                     )
                 column = gate * UNIT_CHUNKS + c
                 nc.scalar.activation(
-                    out=result[:, c, :], in_=acc[:], func=TANH, bias=bias_col[:, column : column + 1], scale=1.0
+                    out=tanh_of[step][:, c, :], in_=acc[:], func=TANH, bias=bias_col[:, column : column + 1], scale=1.0
                 )
-            tanh_of[step] = result
 
-        def mix(step):
+        def mix(step, part):
             b, gate = divmod(step, GATES)
-            if gate == GATE_Z:
+            if part == 0 and gate == GATE_Z:
                 zs_sb[b] = mixes.tile([P, ROW_TILES * FEATURES], F32, name="zs_sb")
-            else:
+            if part == 0 and gate == GATE_G:
                 gh_sb[b] = mixes.tile([P, ROW_TILES * FEATURES], F32, name="gh_sb")
-            for j in range(ROW_TILES):
+            for j in range(part * ROW_TILES_A_ROUND, (part + 1) * ROW_TILES_A_ROUND):
                 bank = tp_psum.tile([P, FEATURES], F32, name="back_bank", tag="tp")
                 for c in range(UNIT_CHUNKS):
                     nc.tensor.transpose(
@@ -206,12 +211,13 @@ def tile_lstmlayer_pb_t_kernel(tc, X, S, H, Uz, Ug, Wz, Wg, bz, bg, out):
                     nc.gpsimd.tensor_tensor(
                         out=zs_sb[b][:, cols], in0=zs_sb[b][:, cols], in1=gh_sb[b][:, cols], op=ALU.subtract
                     )
-            if gate == GATE_G:
+            if gate == GATE_G and part == ROUNDS - 1:
                 nc.sync.dma_start(out=out_blocks[b], in_=zs_sb[b][:])
 
         weight_q[GATE_Z] = quantise_gate_weights(raw_uz, raw_wz, "z")
-        transpose_operand(0)
-        transpose_operand(1)
+        for q in range(2):
+            for part in range(ROUNDS):
+                transpose_operand(q, part)
         quantise_operand(0)
         quantise_operand(1)
         weight_q[GATE_G] = quantise_gate_weights(raw_ug, raw_wg, "g")
@@ -224,13 +230,15 @@ def tile_lstmlayer_pb_t_kernel(tc, X, S, H, Uz, Ug, Wz, Wg, bz, bg, out):
                     load_x_and_s(b + LOAD_LEAD)
                 if b + LOAD_LEAD - 1 < BLOCKS:
                     h_sb[b + LOAD_LEAD - 1] = load(h_blocks[b + LOAD_LEAD - 1], "h_sb")
-            gate_matmuls(step)
-            if step > 0:
-                mix(step - 1)
             until = min(step + TRANSPOSE_LEAD + 1, OPERANDS)
-            for q in range(transposed, until):
-                transpose_operand(q)
+            for part in range(ROUNDS):
+                gate_matmuls(step, part)
+                if step > 0:
+                    mix(step - 1, part)
+                for q in range(transposed, until):
+                    transpose_operand(q, part)
             for q in range(transposed, until):
                 quantise_operand(q)
             transposed = until
-        mix(STEPS - 1)
+        for part in range(ROUNDS):
+            mix(STEPS - 1, part)

@@ -86,13 +86,8 @@ def tile_lstmlayer_pb_t_kernel(tc, X, S, H, Uz, Ug, Wz, Wg, bz, bg, out):
             nc.vector.quantize_mx(out=codes[:].bitcast(FP8X4), scales=scales[:], in_=grouped_flat)
             return codes, scales
 
-        def quantise_gate_weights(raw_u, raw_w, name):
-            grouped_u = regroup_weight(raw_u)
-            grouped_w = regroup_weight(raw_w)
-            return [
-                quantise(grouped_u[:].rearrange("p n t -> p (n t)"), consts, "u" + name),
-                quantise(grouped_w[:].rearrange("p n t -> p (n t)"), consts, "w" + name),
-            ]
+        def quantise_weight(grouped, name):
+            return quantise(grouped[:].rearrange("p n t -> p (n t)"), consts, name)
 
         ident = consts.tile([P, P], F32, name="ident")
         make_identity(nc, ident[:])
@@ -208,20 +203,29 @@ def tile_lstmlayer_pb_t_kernel(tc, X, S, H, Uz, Ug, Wz, Wg, bz, bg, out):
                         op0=ALU.subtract,
                         op1=ALU.mult,
                     )
-                    nc.gpsimd.tensor_tensor(
+                    if b == BLOCKS - 1 and j % 2 == 1:
+                        subtractor = nc.vector
+                    else:
+                        subtractor = nc.gpsimd
+                    subtractor.tensor_tensor(
                         out=zs_sb[b][:, cols], in0=zs_sb[b][:, cols], in1=gh_sb[b][:, cols], op=ALU.subtract
                     )
-            if gate == GATE_G and part == ROUNDS - 1:
-                nc.sync.dma_start(out=out_blocks[b], in_=zs_sb[b][:])
+                    nc.sync.dma_start(out=out_blocks[b][:, cols], in_=zs_sb[b][:, cols])
 
-        weight_q[GATE_Z] = quantise_gate_weights(raw_uz, raw_wz, "z")
         for q in range(2):
             for part in range(ROUNDS):
                 transpose_operand(q, part)
-        quantise_operand(0)
-        quantise_operand(1)
-        weight_q[GATE_G] = quantise_gate_weights(raw_ug, raw_wg, "g")
         transposed = 2
+        grouped_uz = regroup_weight(raw_uz)
+        uz_q = quantise_weight(grouped_uz, "uz")
+        grouped_wz = regroup_weight(raw_wz)
+        quantise_operand(0)
+        wz_q = quantise_weight(grouped_wz, "wz")
+        quantise_operand(1)
+        weight_q[GATE_Z] = [uz_q, wz_q]
+        grouped_ug = regroup_weight(raw_ug)
+        grouped_wg = regroup_weight(raw_wg)
+        weight_q[GATE_G] = [quantise_weight(grouped_ug, "ug"), quantise_weight(grouped_wg, "wg")]
 
         for step in range(STEPS):
             b, gate = divmod(step, GATES)

@@ -21,18 +21,9 @@ BLOCK_ROWS = 512
 ROW_TILES = BLOCK_ROWS // P
 BLOCKS = ROWS // BLOCK_ROWS
 UNIT_CHUNKS = FEATURES // P
-GATE_Z = 0
-GATE_G = 1
-GATES = 2
-STEPS = BLOCKS * GATES
-OPERANDS = BLOCKS * 2
-TRANSPOSE_LEAD = 3
 LOAD_LEAD = 3
-ROUNDS = 2
-CHUNKS_A_ROUND = UNIT_CHUNKS // ROUNDS
-ROW_TILES_A_ROUND = ROW_TILES // ROUNDS
+TRANSPOSE_LEAD = 2
 BANK_ROW_TILES = 2
-IN_BANKS_A_ROUND = ROW_TILES // BANK_ROW_TILES // ROUNDS
 
 FLOPS = 4 * 2 * ROWS * FEATURES * FEATURES
 
@@ -50,8 +41,8 @@ def tile_lstmlayer_pb_t_kernel(tc, X, S, H, Uz, Ug, Wz, Wg, bz, bg, out):
         inputs = ctx.enter_context(tc.tile_pool(name="inputs", bufs=BLOCKS))
         regroup = ctx.enter_context(tc.tile_pool(name="regroup", bufs=2))
         quantised = ctx.enter_context(tc.tile_pool(name="quantised", bufs=4))
-        gates = ctx.enter_context(tc.tile_pool(name="gates", bufs=3))
-        mixes = ctx.enter_context(tc.tile_pool(name="mixes", bufs=2))
+        work = ctx.enter_context(tc.tile_pool(name="work", bufs=2))
+        results = ctx.enter_context(tc.tile_pool(name="results", bufs=3))
         mx_psum = ctx.enter_context(tc.psum_pool(name="mx_psum", bufs=4))
         tp_psum = ctx.enter_context(tc.psum_pool(name="tp_psum", bufs=4))
         ctx.enter_context(tc.manual_schedule())
@@ -96,13 +87,14 @@ def tile_lstmlayer_pb_t_kernel(tc, X, S, H, Uz, Ug, Wz, Wg, bz, bg, out):
         nc.vector.memset(warm[:], 0.0)
         nc.scalar.activation(out=warm[:, 1:2], in_=warm[:, 0:1], func=TANH)
 
-        bias_rows = consts.tile([P, P], BF16, name="bias_rows")
-        nc.vector.memset(bias_rows[:], 0.0)
-        for gate, bias in ((GATE_Z, bz), (GATE_G, bg)):
-            nc.sync.dma_start(
-                out=bias_rows[gate * UNIT_CHUNKS : (gate + 1) * UNIT_CHUNKS, :],
-                in_=bias.rearrange("(c m) -> c m", m=P),
-            )
+        bg_rows = consts.tile([P, P], BF16, name="bg_rows")
+        nc.vector.memset(bg_rows[:], 0.0)
+        nc.sync.dma_start(out=bg_rows[0:UNIT_CHUNKS, :], in_=bg.rearrange("(c m) -> c m", m=P))
+        bz_row = consts.tile([P, FEATURES], BF16, name="bz_row")
+        nc.vector.memset(bz_row[:], 0.0)
+        nc.sync.dma_start(out=bz_row[0:1, :], in_=bz.rearrange("(o m) -> o m", o=1))
+        ones = consts.tile([P, P], BF16, name="ones")
+        nc.vector.memset(ones[:], 1.0)
 
         raw_uz = load_weight(Uz, "raw_uz")
         x_sb[0] = load(x_blocks[0], "x_sb")
@@ -114,26 +106,29 @@ def tile_lstmlayer_pb_t_kernel(tc, X, S, H, Uz, Ug, Wz, Wg, bz, bg, out):
             load_x_and_s(b)
             h_sb[b - 1] = load(h_blocks[b - 1], "h_sb")
 
-        bias_rows_f32 = consts.tile([P, P], F32, name="bias_rows_f32")
-        nc.vector.tensor_copy(out=bias_rows_f32[:], in_=bias_rows[:])
-        bias_bank = tp_psum.tile([P, P], F32, name="bias_bank", tag="tp")
-        nc.tensor.transpose(out=bias_bank[:], in_=bias_rows_f32[:], identity=ident[:])
-        bias_col = consts.tile([P, GATES * UNIT_CHUNKS], F32, name="bias_col")
-        nc.vector.tensor_copy(out=bias_col[:], in_=bias_bank[:, 0 : GATES * UNIT_CHUNKS])
+        bg_rows_f32 = consts.tile([P, P], F32, name="bg_rows_f32")
+        nc.vector.tensor_copy(out=bg_rows_f32[:], in_=bg_rows[:])
+        bg_bank = tp_psum.tile([P, P], F32, name="bg_bank", tag="tp")
+        nc.tensor.transpose(out=bg_bank[:], in_=bg_rows_f32[:], identity=ident[:])
+        bg_col = consts.tile([P, UNIT_CHUNKS], F32, name="bg_col")
+        nc.scalar.copy(out=bg_col[:], in_=bg_bank[:, 0:UNIT_CHUNKS])
+        bz_bank = tp_psum.tile([P, FEATURES], F32, name="bz_bank", tag="tp")
+        nc.tensor.matmul(out=bz_bank[:], lhsT=ones[:], rhs=bz_row[:], start=True, stop=True)
+        bz_full = consts.tile([P, FEATURES], F32, name="bz_full")
+        nc.scalar.copy(out=bz_full[:], in_=bz_bank[:])
 
         grouped_of = {}
         operand_q = {}
-        weight_q = {}
-        tanh_of = {}
-        zs_sb, gh_sb = {}, {}
+        tanh_g = {}
+        z_sb = {}
 
-        def transpose_operand(q, part):
-            source = x_sb[q // 2] if q % 2 == 0 else s_sb[q // 2]
+        def transpose_operand(b, side):
+            source = (x_sb, s_sb)[side][b]
             words = source[:].bitcast(F32)
-            if part == 0:
-                grouped_of[q] = regroup.tile([P, BLOCK_ROWS * PACK], BF16, name="a_grouped", align_bytes=64)
-            grouped_words = grouped_of[q][:].bitcast(F32)
-            for pair in range(part * IN_BANKS_A_ROUND, (part + 1) * IN_BANKS_A_ROUND):
+            grouped = regroup.tile([P, BLOCK_ROWS * PACK], BF16, name="x_grouped" if side == 0 else "s_grouped", align_bytes=64)
+            grouped_of[b, side] = grouped
+            grouped_words = grouped[:].bitcast(F32)
+            for pair in range(ROW_TILES // BANK_ROW_TILES):
                 bank = tp_psum.tile([P, BANK_ROW_TILES, HALVES, P], F32, name="in_bank", tag="tp")
                 for i in range(BANK_ROW_TILES):
                     first = (BANK_ROW_TILES * pair + i) * WORDS
@@ -150,19 +145,45 @@ def tile_lstmlayer_pb_t_kernel(tc, X, S, H, Uz, Ug, Wz, Wg, bz, bg, out):
                     in_=bank[:].rearrange("p i u r -> p i r u"),
                 )
 
-        def quantise_operand(q):
-            operand_q[q] = quantise(grouped_of[q][:], quantised, "a")
+        def quantise_operand(b, side):
+            operand_q[b, side] = quantise(grouped_of[b, side][:], quantised, "a")
 
-        def gate_matmuls(step, part):
-            b, gate = divmod(step, GATES)
-            if part == 0:
-                tanh_of[step] = gates.tile([P, UNIT_CHUNKS, BLOCK_ROWS], F32, name="tanh_sb")
-            for c in range(part * CHUNKS_A_ROUND, (part + 1) * CHUNKS_A_ROUND):
-                units = slice(c * P, (c + 1) * P)
-                acc = mx_psum.tile([P, BLOCK_ROWS], F32, name="acc")
+        def gate_z(b):
+            pre = work.tile([P, ROW_TILES * FEATURES], F32, name="pre")
+            z_sb[b] = results.tile([P, ROW_TILES * FEATURES], F32, name="z_sb")
+            for j in range(ROW_TILES):
+                rows = slice(j * P, (j + 1) * P)
+                cols = slice(j * FEATURES, (j + 1) * FEATURES)
+                acc = mx_psum.tile([P, FEATURES], F32, name="acc_z", tag="mx")
                 for side in range(2):
-                    w_codes, w_scales = weight_q[gate][side]
-                    a_codes, a_scales = operand_q[2 * b + side]
+                    w_codes, w_scales = weight_z[side]
+                    a_codes, a_scales = operand_q[b, side]
+                    nc.tensor.matmul_mx(
+                        out=acc[:],
+                        lhsT=a_codes[:, rows].bitcast(FP8X4),
+                        lhsT_scale=a_scales[:, rows],
+                        rhs=w_codes[:].bitcast(FP8X4),
+                        rhs_scale=w_scales[:],
+                        start=(side == 0),
+                        stop=(side == 1),
+                    )
+                nc.vector.tensor_tensor(out=pre[:, cols], in0=acc[:], in1=bz_full[:], op=ALU.add)
+                if j % 2 == 1:
+                    two = slice((j - 1) * FEATURES, (j + 1) * FEATURES)
+                    nc.scalar.activation(out=z_sb[b][:, two], in_=pre[:, two], func=TANH)
+
+        def times_s(b, j):
+            cols = slice(j * FEATURES, (j + 1) * FEATURES)
+            nc.gpsimd.tensor_tensor(out=z_sb[b][:, cols], in0=z_sb[b][:, cols], in1=s_sb[b][:, cols], op=ALU.mult)
+
+        def gate_g(b):
+            tanh_g[b] = work.tile([P, UNIT_CHUNKS, BLOCK_ROWS], F32, name="tanh_g")
+            for c in range(UNIT_CHUNKS):
+                units = slice(c * P, (c + 1) * P)
+                acc = mx_psum.tile([P, BLOCK_ROWS], F32, name="acc_g", tag="mx")
+                for side in range(2):
+                    w_codes, w_scales = weight_g[side]
+                    a_codes, a_scales = operand_q[b, side]
                     nc.tensor.matmul_mx(
                         out=acc[:],
                         lhsT=w_codes[:, units].bitcast(FP8X4),
@@ -172,77 +193,84 @@ def tile_lstmlayer_pb_t_kernel(tc, X, S, H, Uz, Ug, Wz, Wg, bz, bg, out):
                         start=(side == 0),
                         stop=(side == 1),
                     )
-                column = gate * UNIT_CHUNKS + c
                 nc.scalar.activation(
-                    out=tanh_of[step][:, c, :], in_=acc[:], func=TANH, bias=bias_col[:, column : column + 1], scale=1.0
+                    out=tanh_g[b][:, c, :], in_=acc[:], func=TANH, bias=bg_col[:, c : c + 1], scale=1.0
                 )
 
-        def mix(step, part):
-            b, gate = divmod(step, GATES)
-            if part == 0 and gate == GATE_Z:
-                zs_sb[b] = mixes.tile([P, ROW_TILES * FEATURES], F32, name="zs_sb")
-            if part == 0 and gate == GATE_G:
-                gh_sb[b] = mixes.tile([P, ROW_TILES * FEATURES], F32, name="gh_sb")
-            for j in range(part * ROW_TILES_A_ROUND, (part + 1) * ROW_TILES_A_ROUND):
-                bank = tp_psum.tile([P, FEATURES], F32, name="back_bank", tag="tp")
-                for c in range(UNIT_CHUNKS):
-                    nc.tensor.transpose(
-                        out=bank[:, c * P : (c + 1) * P],
-                        in_=tanh_of[step][:, c, j * P : (j + 1) * P],
-                        identity=ident[:],
-                    )
-                cols = slice(j * FEATURES, (j + 1) * FEATURES)
-                if gate == GATE_Z:
-                    nc.vector.tensor_tensor(out=zs_sb[b][:, cols], in0=bank[:], in1=s_sb[b][:, cols], op=ALU.mult)
-                else:
-                    nc.vector.scalar_tensor_tensor(
-                        out=gh_sb[b][:, cols],
-                        in0=bank[:],
-                        scalar=1.0,
-                        in1=h_sb[b][:, cols],
-                        op0=ALU.subtract,
-                        op1=ALU.mult,
-                    )
-                    if b == BLOCKS - 1 and j % 2 == 1:
-                        subtractor = nc.vector
-                    else:
-                        subtractor = nc.gpsimd
-                    subtractor.tensor_tensor(
-                        out=zs_sb[b][:, cols], in0=zs_sb[b][:, cols], in1=gh_sb[b][:, cols], op=ALU.subtract
-                    )
-                    nc.sync.dma_start(out=out_blocks[b][:, cols], in_=zs_sb[b][:, cols])
+        gh_of = {}
 
-        for q in range(2):
-            for part in range(ROUNDS):
-                transpose_operand(q, part)
-        transposed = 2
+        def g_times_h(b, j):
+            if j == 0:
+                gh_of[b] = work.tile([P, ROW_TILES * FEATURES], F32, name="gh_sb")
+            bank = tp_psum.tile([P, FEATURES], F32, name="back_bank", tag="tp")
+            for c in range(UNIT_CHUNKS):
+                nc.tensor.transpose(
+                    out=bank[:, c * P : (c + 1) * P],
+                    in_=tanh_g[b][:, c, j * P : (j + 1) * P],
+                    identity=ident[:],
+                )
+            cols = slice(j * FEATURES, (j + 1) * FEATURES)
+            nc.vector.scalar_tensor_tensor(
+                out=gh_of[b][:, cols],
+                in0=bank[:],
+                scalar=1.0,
+                in1=h_sb[b][:, cols],
+                op0=ALU.subtract,
+                op1=ALU.mult,
+            )
+
+        def finish(engine, b, j):
+            cols = slice(j * FEATURES, (j + 1) * FEATURES)
+            engine.tensor_tensor(out=z_sb[b][:, cols], in0=z_sb[b][:, cols], in1=gh_of[b][:, cols], op=ALU.subtract)
+            nc.sync.dma_start(out=out_blocks[b][:, cols], in_=z_sb[b][:, cols])
+
+        for side in range(2):
+            transpose_operand(0, side)
         grouped_uz = regroup_weight(raw_uz)
         uz_q = quantise_weight(grouped_uz, "uz")
         grouped_wz = regroup_weight(raw_wz)
-        quantise_operand(0)
+        quantise_operand(0, 0)
         wz_q = quantise_weight(grouped_wz, "wz")
-        quantise_operand(1)
-        weight_q[GATE_Z] = [uz_q, wz_q]
+        quantise_operand(0, 1)
+        weight_z = [uz_q, wz_q]
         grouped_ug = regroup_weight(raw_ug)
         grouped_wg = regroup_weight(raw_wg)
-        weight_q[GATE_G] = [quantise_weight(grouped_ug, "ug"), quantise_weight(grouped_wg, "wg")]
+        weight_g = [quantise_weight(grouped_ug, "ug"), quantise_weight(grouped_wg, "wg")]
 
-        for step in range(STEPS):
-            b, gate = divmod(step, GATES)
-            if gate == GATE_Z:
-                if b + LOAD_LEAD < BLOCKS:
-                    load_x_and_s(b + LOAD_LEAD)
-                if b + LOAD_LEAD - 1 < BLOCKS:
-                    h_sb[b + LOAD_LEAD - 1] = load(h_blocks[b + LOAD_LEAD - 1], "h_sb")
-            until = min(step + TRANSPOSE_LEAD + 1, OPERANDS)
-            for part in range(ROUNDS):
-                gate_matmuls(step, part)
-                if step > 0:
-                    mix(step - 1, part)
-                for q in range(transposed, until):
-                    transpose_operand(q, part)
-            for q in range(transposed, until):
-                quantise_operand(q)
-            transposed = until
-        for part in range(ROUNDS):
-            mix(STEPS - 1, part)
+        for b in range(BLOCKS):
+            if b + LOAD_LEAD < BLOCKS:
+                load_x_and_s(b + LOAD_LEAD)
+            if b + LOAD_LEAD - 1 < BLOCKS:
+                h_sb[b + LOAD_LEAD - 1] = load(h_blocks[b + LOAD_LEAD - 1], "h_sb")
+
+            gate_z(b)
+            if b == 0:
+                for side in range(2):
+                    transpose_operand(1, side)
+            else:
+                for j in range(ROW_TILES):
+                    g_times_h(b - 1, j)
+            if b + 1 < BLOCKS:
+                for side in range(2):
+                    quantise_operand(b + 1, side)
+            times_s(b, 0)
+            times_s(b, 1)
+            if b > 0:
+                finish(nc.vector, b - 1, 0)
+                finish(nc.vector, b - 1, 1)
+                finish(nc.gpsimd, b - 1, 2)
+                finish(nc.gpsimd, b - 1, 3)
+            times_s(b, 2)
+            times_s(b, 3)
+
+            gate_g(b)
+            if b + TRANSPOSE_LEAD < BLOCKS:
+                for side in range(2):
+                    transpose_operand(b + TRANSPOSE_LEAD, side)
+
+        last = BLOCKS - 1
+        for j in range(0, ROW_TILES, 2):
+            g_times_h(last, j)
+            g_times_h(last, j + 1)
+            finish(nc.gpsimd, last, j)
+            finish(nc.vector, last, j + 1)

@@ -42,7 +42,8 @@ def tile_lstmlayer_pb_t_kernel(tc, X, S, H, Uz, Ug, Wz, Wg, bz, bg, out):
         regroup = ctx.enter_context(tc.tile_pool(name="regroup", bufs=2))
         quantised = ctx.enter_context(tc.tile_pool(name="quantised", bufs=4))
         work = ctx.enter_context(tc.tile_pool(name="work", bufs=2))
-        results = ctx.enter_context(tc.tile_pool(name="results", bufs=3))
+        pres = ctx.enter_context(tc.tile_pool(name="pres", bufs=1))
+        results = ctx.enter_context(tc.tile_pool(name="results", bufs=4))
         mx_psum = ctx.enter_context(tc.psum_pool(name="mx_psum", bufs=4))
         tp_psum = ctx.enter_context(tc.psum_pool(name="tp_psum", bufs=4))
         ctx.enter_context(tc.manual_schedule())
@@ -120,6 +121,12 @@ def tile_lstmlayer_pb_t_kernel(tc, X, S, H, Uz, Ug, Wz, Wg, bz, bg, out):
         grouped_of = {}
         operand_q = {}
         tanh_g = {}
+        pre_of = {}
+        halves = [range(0, 2), range(2, 4)]
+
+        def half_cols(part):
+            return slice(part * 2 * FEATURES, (part + 1) * 2 * FEATURES)
+
         z_sb = {}
 
         def transpose_operand(b, side):
@@ -148,10 +155,12 @@ def tile_lstmlayer_pb_t_kernel(tc, X, S, H, Uz, Ug, Wz, Wg, bz, bg, out):
         def quantise_operand(b, side):
             operand_q[b, side] = quantise(grouped_of[b, side][:], quantised, "a")
 
-        def gate_z(b):
-            pre = work.tile([P, ROW_TILES * FEATURES], F32, name="pre")
-            z_sb[b] = results.tile([P, ROW_TILES * FEATURES], F32, name="z_sb")
-            for j in range(ROW_TILES):
+        def gate_z(b, part):
+            if part == 0:
+                pre_of[b] = pres.tile([P, ROW_TILES * FEATURES], F32, name="pre")
+                z_sb[b] = results.tile([P, ROW_TILES * FEATURES], F32, name="z_sb")
+            pre = pre_of[b]
+            for j in halves[part]:
                 rows = slice(j * P, (j + 1) * P)
                 cols = slice(j * FEATURES, (j + 1) * FEATURES)
                 acc = mx_psum.tile([P, FEATURES], F32, name="acc_z", tag="mx")
@@ -168,17 +177,17 @@ def tile_lstmlayer_pb_t_kernel(tc, X, S, H, Uz, Ug, Wz, Wg, bz, bg, out):
                         stop=(side == 1),
                     )
                 nc.vector.tensor_tensor(out=pre[:, cols], in0=acc[:], in1=bz_full[:], op=ALU.add)
-                if j % 2 == 1:
-                    two = slice((j - 1) * FEATURES, (j + 1) * FEATURES)
-                    nc.scalar.activation(out=z_sb[b][:, two], in_=pre[:, two], func=TANH)
+            cols = half_cols(part)
+            nc.scalar.activation(out=z_sb[b][:, cols], in_=pre[:, cols], func=TANH)
 
-        def times_s(b, j):
-            cols = slice(j * FEATURES, (j + 1) * FEATURES)
-            nc.gpsimd.tensor_tensor(out=z_sb[b][:, cols], in0=z_sb[b][:, cols], in1=s_sb[b][:, cols], op=ALU.mult)
+        def times_s(b, part):
+            cols = half_cols(part)
+            nc.vector.tensor_tensor(out=z_sb[b][:, cols], in0=z_sb[b][:, cols], in1=s_sb[b][:, cols], op=ALU.mult)
 
-        def gate_g(b):
-            tanh_g[b] = work.tile([P, UNIT_CHUNKS, BLOCK_ROWS], F32, name="tanh_g")
-            for c in range(UNIT_CHUNKS):
+        def gate_g(b, part):
+            if part == 0:
+                tanh_g[b] = work.tile([P, UNIT_CHUNKS, BLOCK_ROWS], F32, name="tanh_g")
+            for c in halves[part]:
                 units = slice(c * P, (c + 1) * P)
                 acc = mx_psum.tile([P, BLOCK_ROWS], F32, name="acc_g", tag="mx")
                 for side in range(2):
@@ -243,32 +252,34 @@ def tile_lstmlayer_pb_t_kernel(tc, X, S, H, Uz, Ug, Wz, Wg, bz, bg, out):
             if b + LOAD_LEAD - 1 < BLOCKS:
                 h_sb[b + LOAD_LEAD - 1] = load(h_blocks[b + LOAD_LEAD - 1], "h_sb")
 
-            gate_z(b)
-            if b == 0:
-                for side in range(2):
-                    transpose_operand(1, side)
-            else:
+            for part in range(2):
+                gate_z(b, part)
+                if b == 0:
+                    transpose_operand(1, part)
+                else:
+                    for j in halves[part]:
+                        g_times_h(b - 1, j)
+            if b > 1:
                 for j in range(ROW_TILES):
-                    g_times_h(b - 1, j)
+                    finish(nc.gpsimd, b - 2, j)
             if b + 1 < BLOCKS:
                 for side in range(2):
                     quantise_operand(b + 1, side)
-            times_s(b, 0)
-            times_s(b, 1)
             if b > 0:
-                finish(nc.vector, b - 1, 0)
-                finish(nc.vector, b - 1, 1)
-                finish(nc.gpsimd, b - 1, 2)
-                finish(nc.gpsimd, b - 1, 3)
-            times_s(b, 2)
-            times_s(b, 3)
+                times_s(b - 1, 1)
+                times_s(b - 1, 0)
 
-            gate_g(b)
-            if b + TRANSPOSE_LEAD < BLOCKS:
-                for side in range(2):
-                    transpose_operand(b + TRANSPOSE_LEAD, side)
+            for part in range(2):
+                gate_g(b, part)
+                if b + TRANSPOSE_LEAD < BLOCKS:
+                    transpose_operand(b + TRANSPOSE_LEAD, part)
 
         last = BLOCKS - 1
+        times_s(last, 0)
+        times_s(last, 1)
+        for j in range(0, ROW_TILES, 2):
+            finish(nc.gpsimd, last - 1, j)
+            finish(nc.vector, last - 1, j + 1)
         for j in range(0, ROW_TILES, 2):
             g_times_h(last, j)
             g_times_h(last, j + 1)

@@ -24,6 +24,11 @@ UNIT_CHUNKS = FEATURES // P
 LOAD_LEAD = 3
 TRANSPOSE_LEAD = 2
 BANK_ROW_TILES = 2
+Z_BY_ROWS = range(0, 2)
+Z_BY_UNITS = range(2, 4)
+Z_COLS = 256
+GATE_Z = 0
+GATE_G = 1
 
 FLOPS = 4 * 2 * ROWS * FEATURES * FEATURES
 
@@ -42,8 +47,8 @@ def tile_lstmlayer_pb_t_kernel(tc, X, S, H, Uz, Ug, Wz, Wg, bz, bg, out):
         regroup = ctx.enter_context(tc.tile_pool(name="regroup", bufs=2))
         quantised = ctx.enter_context(tc.tile_pool(name="quantised", bufs=4))
         work = ctx.enter_context(tc.tile_pool(name="work", bufs=2))
-        pres = ctx.enter_context(tc.tile_pool(name="pres", bufs=1))
-        results = ctx.enter_context(tc.tile_pool(name="results", bufs=4))
+        pres = ctx.enter_context(tc.tile_pool(name="pres", bufs=2))
+        results = ctx.enter_context(tc.tile_pool(name="results", bufs=3))
         mx_psum = ctx.enter_context(tc.psum_pool(name="mx_psum", bufs=4))
         tp_psum = ctx.enter_context(tc.psum_pool(name="tp_psum", bufs=4))
         ctx.enter_context(tc.manual_schedule())
@@ -67,9 +72,9 @@ def tile_lstmlayer_pb_t_kernel(tc, X, S, H, Uz, Ug, Wz, Wg, bz, bg, out):
             )
             return raw
 
-        def regroup_weight(raw):
+        def regroup_weight(copy, raw):
             grouped = regroup.tile([P, FEATURES, PACK], BF16, name="w_grouped", align_bytes=64)
-            nc.vector.tensor_copy(out=grouped[:], in_=raw[:].rearrange("p t n -> p n t"))
+            copy(out=grouped[:], in_=raw[:].rearrange("p t n -> p n t"))
             return grouped
 
         def quantise(grouped_flat, pool, name):
@@ -88,9 +93,13 @@ def tile_lstmlayer_pb_t_kernel(tc, X, S, H, Uz, Ug, Wz, Wg, bz, bg, out):
         nc.vector.memset(warm[:], 0.0)
         nc.scalar.activation(out=warm[:, 1:2], in_=warm[:, 0:1], func=TANH)
 
-        bg_rows = consts.tile([P, P], BF16, name="bg_rows")
-        nc.vector.memset(bg_rows[:], 0.0)
-        nc.sync.dma_start(out=bg_rows[0:UNIT_CHUNKS, :], in_=bg.rearrange("(c m) -> c m", m=P))
+        bias_rows = consts.tile([P, P], BF16, name="bias_rows")
+        nc.vector.memset(bias_rows[:], 0.0)
+        for gate, bias in ((GATE_Z, bz), (GATE_G, bg)):
+            nc.sync.dma_start(
+                out=bias_rows[gate * UNIT_CHUNKS : (gate + 1) * UNIT_CHUNKS, :],
+                in_=bias.rearrange("(c m) -> c m", m=P),
+            )
         bz_row = consts.tile([P, FEATURES], BF16, name="bz_row")
         nc.vector.memset(bz_row[:], 0.0)
         nc.sync.dma_start(out=bz_row[0:1, :], in_=bz.rearrange("(o m) -> o m", o=1))
@@ -107,12 +116,12 @@ def tile_lstmlayer_pb_t_kernel(tc, X, S, H, Uz, Ug, Wz, Wg, bz, bg, out):
             load_x_and_s(b)
             h_sb[b - 1] = load(h_blocks[b - 1], "h_sb")
 
-        bg_rows_f32 = consts.tile([P, P], F32, name="bg_rows_f32")
-        nc.vector.tensor_copy(out=bg_rows_f32[:], in_=bg_rows[:])
-        bg_bank = tp_psum.tile([P, P], F32, name="bg_bank", tag="tp")
-        nc.tensor.transpose(out=bg_bank[:], in_=bg_rows_f32[:], identity=ident[:])
-        bg_col = consts.tile([P, UNIT_CHUNKS], F32, name="bg_col")
-        nc.scalar.copy(out=bg_col[:], in_=bg_bank[:, 0:UNIT_CHUNKS])
+        bias_rows_f32 = consts.tile([P, P], F32, name="bias_rows_f32")
+        nc.vector.tensor_copy(out=bias_rows_f32[:], in_=bias_rows[:])
+        bias_bank = tp_psum.tile([P, P], F32, name="bias_bank", tag="tp")
+        nc.tensor.transpose(out=bias_bank[:], in_=bias_rows_f32[:], identity=ident[:])
+        bias_col = consts.tile([P, 2 * UNIT_CHUNKS], F32, name="bias_col")
+        nc.scalar.copy(out=bias_col[:], in_=bias_bank[:, 0 : 2 * UNIT_CHUNKS])
         bz_bank = tp_psum.tile([P, FEATURES], F32, name="bz_bank", tag="tp")
         nc.tensor.matmul(out=bz_bank[:], lhsT=ones[:], rhs=bz_row[:], start=True, stop=True)
         bz_full = consts.tile([P, FEATURES], F32, name="bz_full")
@@ -121,165 +130,184 @@ def tile_lstmlayer_pb_t_kernel(tc, X, S, H, Uz, Ug, Wz, Wg, bz, bg, out):
         grouped_of = {}
         operand_q = {}
         tanh_g = {}
-        pre_of = {}
-        halves = [range(0, 2), range(2, 4)]
-
-        def half_cols(part):
-            return slice(part * 2 * FEATURES, (part + 1) * 2 * FEATURES)
-
+        tanh_z = {}
+        gh_sb = {}
         z_sb = {}
+        rows_cols = slice(0, len(Z_BY_ROWS) * FEATURES)
 
-        def transpose_operand(b, side):
+        def cols_of(j):
+            return slice(j * FEATURES, (j + 1) * FEATURES)
+
+        def transpose_operand(b, side, pair):
             source = (x_sb, s_sb)[side][b]
             words = source[:].bitcast(F32)
-            grouped = regroup.tile([P, BLOCK_ROWS * PACK], BF16, name="x_grouped" if side == 0 else "s_grouped", align_bytes=64)
-            grouped_of[b, side] = grouped
-            grouped_words = grouped[:].bitcast(F32)
-            for pair in range(ROW_TILES // BANK_ROW_TILES):
-                bank = tp_psum.tile([P, BANK_ROW_TILES, HALVES, P], F32, name="in_bank", tag="tp")
-                for i in range(BANK_ROW_TILES):
-                    first = (BANK_ROW_TILES * pair + i) * WORDS
-                    for u in range(HALVES):
-                        nc.tensor.transpose(
-                            out=bank[:, i, u, :],
-                            in_=words[:, first + u * P : first + (u + 1) * P],
-                            identity=ident[:],
-                        )
-                nc.scalar.copy(
-                    out=grouped_words[:, pair * BANK_ROW_TILES * WORDS : (pair + 1) * BANK_ROW_TILES * WORDS].rearrange(
-                        "p (i r u) -> p i r u", i=BANK_ROW_TILES, u=HALVES
-                    ),
-                    in_=bank[:].rearrange("p i u r -> p i r u"),
+            if pair == 0:
+                grouped_of[b, side] = regroup.tile(
+                    [P, BLOCK_ROWS * PACK], BF16, name=("x_grouped", "s_grouped")[side], align_bytes=64
                 )
+            grouped_words = grouped_of[b, side][:].bitcast(F32)
+            bank = tp_psum.tile([P, BANK_ROW_TILES, HALVES, P], F32, name="in_bank", tag="tp")
+            for i in range(BANK_ROW_TILES):
+                first = (BANK_ROW_TILES * pair + i) * WORDS
+                for u in range(HALVES):
+                    nc.tensor.transpose(
+                        out=bank[:, i, u, :],
+                        in_=words[:, first + u * P : first + (u + 1) * P],
+                        identity=ident[:],
+                    )
+            nc.scalar.copy(
+                out=grouped_words[:, pair * BANK_ROW_TILES * WORDS : (pair + 1) * BANK_ROW_TILES * WORDS].rearrange(
+                    "p (i r u) -> p i r u", i=BANK_ROW_TILES, u=HALVES
+                ),
+                in_=bank[:].rearrange("p i u r -> p i r u"),
+            )
 
         def quantise_operand(b, side):
-            operand_q[b, side] = quantise(grouped_of[b, side][:], quantised, "a")
+            return quantise(grouped_of[b, side][:], quantised, "a")
 
-        def gate_z(b, part):
-            if part == 0:
-                pre_of[b] = pres.tile([P, ROW_TILES * FEATURES], F32, name="pre")
-                z_sb[b] = results.tile([P, ROW_TILES * FEATURES], F32, name="z_sb")
-            pre = pre_of[b]
-            for j in halves[part]:
-                rows = slice(j * P, (j + 1) * P)
-                cols = slice(j * FEATURES, (j + 1) * FEATURES)
-                acc = mx_psum.tile([P, FEATURES], F32, name="acc_z", tag="mx")
-                for side in range(2):
-                    w_codes, w_scales = weight_z[side]
-                    a_codes, a_scales = operand_q[b, side]
-                    nc.tensor.matmul_mx(
-                        out=acc[:],
-                        lhsT=a_codes[:, rows].bitcast(FP8X4),
-                        lhsT_scale=a_scales[:, rows],
-                        rhs=w_codes[:].bitcast(FP8X4),
-                        rhs_scale=w_scales[:],
-                        start=(side == 0),
-                        stop=(side == 1),
-                    )
-                nc.vector.tensor_tensor(out=pre[:, cols], in0=acc[:], in1=bz_full[:], op=ALU.add)
-            cols = half_cols(part)
-            nc.scalar.activation(out=z_sb[b][:, cols], in_=pre[:, cols], func=TANH)
+        def two_passes(acc, stationary, units_or_rows, moving, columns):
+            for side in range(2):
+                l_codes, l_scales = stationary[side]
+                r_codes, r_scales = moving[side]
+                nc.tensor.matmul_mx(
+                    out=acc,
+                    lhsT=l_codes[:, units_or_rows].bitcast(FP8X4),
+                    lhsT_scale=l_scales[:, units_or_rows],
+                    rhs=r_codes[:, columns].bitcast(FP8X4),
+                    rhs_scale=r_scales[:, columns],
+                    start=(side == 0),
+                    stop=(side == 1),
+                )
 
-        def times_s(b, part):
-            cols = half_cols(part)
-            nc.vector.tensor_tensor(out=z_sb[b][:, cols], in0=z_sb[b][:, cols], in1=s_sb[b][:, cols], op=ALU.mult)
+        def gate_z_by_rows(b):
+            pre = pres.tile([P, len(Z_BY_ROWS) * FEATURES], F32, name="pre")
+            z_sb[b] = results.tile([P, ROW_TILES * FEATURES], F32, name="z_sb")
+            for j in Z_BY_ROWS:
+                acc = mx_psum.tile([P, FEATURES], F32, name="acc_rows", tag="mx")
+                two_passes(acc[:], operand_q[b], slice(j * P, (j + 1) * P), weight_q[GATE_Z], slice(0, FEATURES))
+                nc.vector.tensor_tensor(out=pre[:, cols_of(j)], in0=acc[:], in1=bz_full[:], op=ALU.add)
+            return pre
+
+        def tanh_z_by_rows(b, pre):
+            nc.scalar.activation(out=z_sb[b][:, rows_cols], in_=pre[:], func=TANH)
+
+        def gate_z_by_units(b):
+            tanh_z[b] = work.tile([P, UNIT_CHUNKS, Z_COLS], F32, name="tanh_z")
+            for c in range(UNIT_CHUNKS):
+                if c % 2 == 0:
+                    acc = mx_psum.tile([P, 2, Z_COLS], F32, name="acc_z", tag="mx")
+                columns = slice(BLOCK_ROWS - Z_COLS, BLOCK_ROWS)
+                two_passes(acc[:, c % 2, :], weight_q[GATE_Z], slice(c * P, (c + 1) * P), operand_q[b], columns)
+                if c % 2 == 1:
+                    for i in range(2):
+                        column = GATE_Z * UNIT_CHUNKS + c - 1 + i
+                        nc.scalar.activation(
+                            out=tanh_z[b][:, c - 1 + i, :],
+                            in_=acc[:, i, :],
+                            func=TANH,
+                            bias=bias_col[:, column : column + 1],
+                            scale=1.0,
+                        )
 
         def gate_g(b, part):
             if part == 0:
                 tanh_g[b] = work.tile([P, UNIT_CHUNKS, BLOCK_ROWS], F32, name="tanh_g")
-            for c in halves[part]:
-                units = slice(c * P, (c + 1) * P)
+            for c in range(2 * part, 2 * part + 2):
                 acc = mx_psum.tile([P, BLOCK_ROWS], F32, name="acc_g", tag="mx")
-                for side in range(2):
-                    w_codes, w_scales = weight_g[side]
-                    a_codes, a_scales = operand_q[b, side]
-                    nc.tensor.matmul_mx(
-                        out=acc[:],
-                        lhsT=w_codes[:, units].bitcast(FP8X4),
-                        lhsT_scale=w_scales[:, units],
-                        rhs=a_codes[:].bitcast(FP8X4),
-                        rhs_scale=a_scales[:],
-                        start=(side == 0),
-                        stop=(side == 1),
-                    )
+                two_passes(acc[:], weight_q[GATE_G], slice(c * P, (c + 1) * P), operand_q[b], slice(0, BLOCK_ROWS))
+                column = GATE_G * UNIT_CHUNKS + c
                 nc.scalar.activation(
-                    out=tanh_g[b][:, c, :], in_=acc[:], func=TANH, bias=bg_col[:, c : c + 1], scale=1.0
+                    out=tanh_g[b][:, c, :], in_=acc[:], func=TANH, bias=bias_col[:, column : column + 1], scale=1.0
                 )
 
-        gh_of = {}
-
-        def g_times_h(b, j):
-            if j == 0:
-                gh_of[b] = work.tile([P, ROW_TILES * FEATURES], F32, name="gh_sb")
+        def transpose_back(source, first):
             bank = tp_psum.tile([P, FEATURES], F32, name="back_bank", tag="tp")
             for c in range(UNIT_CHUNKS):
                 nc.tensor.transpose(
-                    out=bank[:, c * P : (c + 1) * P],
-                    in_=tanh_g[b][:, c, j * P : (j + 1) * P],
-                    identity=ident[:],
+                    out=bank[:, c * P : (c + 1) * P], in_=source[:, c, first : first + P], identity=ident[:]
                 )
-            cols = slice(j * FEATURES, (j + 1) * FEATURES)
+            return bank
+
+        def z_times_s_by_units(b, j):
+            bank = transpose_back(tanh_z[b], (j - Z_BY_UNITS.start) * P)
+            nc.vector.tensor_tensor(out=z_sb[b][:, cols_of(j)], in0=bank[:], in1=s_sb[b][:, cols_of(j)], op=ALU.mult)
+
+        def z_times_s_by_rows(b):
+            nc.vector.tensor_tensor(
+                out=z_sb[b][:, rows_cols], in0=z_sb[b][:, rows_cols], in1=s_sb[b][:, rows_cols], op=ALU.mult
+            )
+
+        def g_times_h(b, j):
+            if j == 0:
+                gh_sb[b] = work.tile([P, ROW_TILES * FEATURES], F32, name="gh_sb")
+            bank = transpose_back(tanh_g[b], j * P)
             nc.vector.scalar_tensor_tensor(
-                out=gh_of[b][:, cols],
+                out=gh_sb[b][:, cols_of(j)],
                 in0=bank[:],
                 scalar=1.0,
-                in1=h_sb[b][:, cols],
+                in1=h_sb[b][:, cols_of(j)],
                 op0=ALU.subtract,
                 op1=ALU.mult,
             )
 
         def finish(engine, b, j):
-            cols = slice(j * FEATURES, (j + 1) * FEATURES)
-            engine.tensor_tensor(out=z_sb[b][:, cols], in0=z_sb[b][:, cols], in1=gh_of[b][:, cols], op=ALU.subtract)
+            cols = cols_of(j)
+            engine.tensor_tensor(out=z_sb[b][:, cols], in0=z_sb[b][:, cols], in1=gh_sb[b][:, cols], op=ALU.subtract)
             nc.sync.dma_start(out=out_blocks[b][:, cols], in_=z_sb[b][:, cols])
 
         for side in range(2):
-            transpose_operand(0, side)
-        grouped_uz = regroup_weight(raw_uz)
+            for pair in range(2):
+                transpose_operand(0, side, pair)
+        grouped_uz = regroup_weight(nc.vector.tensor_copy, raw_uz)
         uz_q = quantise_weight(grouped_uz, "uz")
-        grouped_wz = regroup_weight(raw_wz)
-        quantise_operand(0, 0)
+        grouped_wz = regroup_weight(nc.vector.tensor_copy, raw_wz)
+        x0_q = quantise_operand(0, 0)
         wz_q = quantise_weight(grouped_wz, "wz")
-        quantise_operand(0, 1)
-        weight_z = [uz_q, wz_q]
-        grouped_ug = regroup_weight(raw_ug)
-        grouped_wg = regroup_weight(raw_wg)
-        weight_g = [quantise_weight(grouped_ug, "ug"), quantise_weight(grouped_wg, "wg")]
+        operand_q[0] = [x0_q, quantise_operand(0, 1)]
+        weight_q = {GATE_Z: [uz_q, wz_q]}
+        grouped_ug = regroup_weight(nc.scalar.copy, raw_ug)
+        grouped_wg = regroup_weight(nc.vector.tensor_copy, raw_wg)
 
         for b in range(BLOCKS):
             if b + LOAD_LEAD < BLOCKS:
                 load_x_and_s(b + LOAD_LEAD)
             if b + LOAD_LEAD - 1 < BLOCKS:
                 h_sb[b + LOAD_LEAD - 1] = load(h_blocks[b + LOAD_LEAD - 1], "h_sb")
+            ahead = b + TRANSPOSE_LEAD
 
-            for part in range(2):
-                gate_z(b, part)
-                if b == 0:
-                    transpose_operand(1, part)
-                else:
-                    for j in halves[part]:
-                        g_times_h(b - 1, j)
-            if b > 1:
-                for j in range(ROW_TILES):
-                    finish(nc.gpsimd, b - 2, j)
-            if b + 1 < BLOCKS:
+            pre = gate_z_by_rows(b)
+            gate_z_by_units(b)
+            tanh_z_by_rows(b, pre)
+            if b == 0:
+                weight_q[GATE_G] = [quantise_weight(grouped_ug, "ug"), quantise_weight(grouped_wg, "wg")]
                 for side in range(2):
-                    quantise_operand(b + 1, side)
-            if b > 0:
-                times_s(b - 1, 1)
-                times_s(b - 1, 0)
+                    for pair in range(2):
+                        transpose_operand(1, side, pair)
+            else:
+                for j in range(ROW_TILES):
+                    g_times_h(b - 1, j)
+                finish(nc.gpsimd, b - 1, 2)
+                finish(nc.gpsimd, b - 1, 3)
 
-            for part in range(2):
-                gate_g(b, part)
-                if b + TRANSPOSE_LEAD < BLOCKS:
-                    transpose_operand(b + TRANSPOSE_LEAD, part)
+            gate_g(b, 0)
+            for j in Z_BY_UNITS:
+                z_times_s_by_units(b, j)
+            if ahead < BLOCKS:
+                transpose_operand(ahead, 0, 0)
+            if b + 1 < BLOCKS:
+                operand_q[b + 1] = [quantise_operand(b + 1, side) for side in range(2)]
+            z_times_s_by_rows(b)
+            if b > 0:
+                finish(nc.vector, b - 1, 0)
+                finish(nc.vector, b - 1, 1)
+
+            gate_g(b, 1)
+            if ahead < BLOCKS:
+                transpose_operand(ahead, 0, 1)
+                for pair in range(2):
+                    transpose_operand(ahead, 1, pair)
 
         last = BLOCKS - 1
-        times_s(last, 0)
-        times_s(last, 1)
-        for j in range(0, ROW_TILES, 2):
-            finish(nc.gpsimd, last - 1, j)
-            finish(nc.vector, last - 1, j + 1)
         for j in range(0, ROW_TILES, 2):
             g_times_h(last, j)
             g_times_h(last, j + 1)

@@ -77,6 +77,9 @@ def tile_lstmlayer_pb_t_kernel(tc, X, S, H, Uz, Ug, Wz, Wg, bz, bg, out):
             copy(out=grouped[:], in_=raw[:].rearrange("p t n -> p n t"))
             return grouped
 
+        def gpsimd_copy(out, in_):
+            nc.gpsimd.tensor_scalar(out=out, in0=in_, scalar1=1.0, scalar2=0.0, op0=ALU.mult, op1=ALU.add)
+
         def quantise(grouped_flat, pool, name):
             codes = pool.tile([P, FEATURES], U32, name=name + "_codes", align_bytes=64)
             scales = pool.tile([P, FEATURES], U8, name=name + "_scales", align_bytes=64)
@@ -115,17 +118,6 @@ def tile_lstmlayer_pb_t_kernel(tc, X, S, H, Uz, Ug, Wz, Wg, bz, bg, out):
         for b in range(1, LOAD_LEAD):
             load_x_and_s(b)
             h_sb[b - 1] = load(h_blocks[b - 1], "h_sb")
-
-        bias_rows_f32 = consts.tile([P, P], F32, name="bias_rows_f32")
-        nc.vector.tensor_copy(out=bias_rows_f32[:], in_=bias_rows[:])
-        bias_bank = tp_psum.tile([P, P], F32, name="bias_bank", tag="tp")
-        nc.tensor.transpose(out=bias_bank[:], in_=bias_rows_f32[:], identity=ident[:])
-        bias_col = consts.tile([P, 2 * UNIT_CHUNKS], F32, name="bias_col")
-        nc.scalar.copy(out=bias_col[:], in_=bias_bank[:, 0 : 2 * UNIT_CHUNKS])
-        bz_bank = tp_psum.tile([P, FEATURES], F32, name="bz_bank", tag="tp")
-        nc.tensor.matmul(out=bz_bank[:], lhsT=ones[:], rhs=bz_row[:], start=True, stop=True)
-        bz_full = consts.tile([P, FEATURES], F32, name="bz_full")
-        nc.scalar.copy(out=bz_full[:], in_=bz_bank[:])
 
         grouped_of = {}
         operand_q = {}
@@ -255,18 +247,31 @@ def tile_lstmlayer_pb_t_kernel(tc, X, S, H, Uz, Ug, Wz, Wg, bz, bg, out):
             engine.tensor_tensor(out=z_sb[b][:, cols], in0=z_sb[b][:, cols], in1=gh_sb[b][:, cols], op=ALU.subtract)
             nc.sync.dma_start(out=out_blocks[b][:, cols], in_=z_sb[b][:, cols])
 
-        for side in range(2):
-            for pair in range(2):
-                transpose_operand(0, side, pair)
+        bias_rows_f32 = consts.tile([P, P], F32, name="bias_rows_f32")
+        nc.scalar.copy(out=bias_rows_f32[:], in_=bias_rows[:])
+        bias_bank = tp_psum.tile([P, P], F32, name="bias_bank", tag="tp")
+        nc.tensor.transpose(out=bias_bank[:], in_=bias_rows_f32[:], identity=ident[:])
+        bias_col = consts.tile([P, 2 * UNIT_CHUNKS], F32, name="bias_col")
+        nc.scalar.copy(out=bias_col[:], in_=bias_bank[:, 0 : 2 * UNIT_CHUNKS])
+        bz_bank = tp_psum.tile([P, FEATURES], F32, name="bz_bank", tag="tp")
+        nc.tensor.matmul(out=bz_bank[:], lhsT=ones[:], rhs=bz_row[:], start=True, stop=True)
+        bz_full = consts.tile([P, FEATURES], F32, name="bz_full")
+        nc.scalar.copy(out=bz_full[:], in_=bz_bank[:])
+
+        for pair in range(2):
+            transpose_operand(0, 0, pair)
+        for pair in range(2):
+            transpose_operand(0, 1, pair)
         grouped_uz = regroup_weight(nc.vector.tensor_copy, raw_uz)
         uz_q = quantise_weight(grouped_uz, "uz")
         grouped_wz = regroup_weight(nc.vector.tensor_copy, raw_wz)
         x0_q = quantise_operand(0, 0)
         wz_q = quantise_weight(grouped_wz, "wz")
-        operand_q[0] = [x0_q, quantise_operand(0, 1)]
+        s0_q = quantise_operand(0, 1)
+        grouped_ug = regroup_weight(gpsimd_copy, raw_ug)
+        grouped_wg = regroup_weight(gpsimd_copy, raw_wg)
+        operand_q[0] = [x0_q, s0_q]
         weight_q = {GATE_Z: [uz_q, wz_q]}
-        grouped_ug = regroup_weight(nc.scalar.copy, raw_ug)
-        grouped_wg = regroup_weight(nc.vector.tensor_copy, raw_wg)
 
         for b in range(BLOCKS):
             if b + LOAD_LEAD < BLOCKS:
@@ -286,8 +291,8 @@ def tile_lstmlayer_pb_t_kernel(tc, X, S, H, Uz, Ug, Wz, Wg, bz, bg, out):
             else:
                 for j in range(ROW_TILES):
                     g_times_h(b - 1, j)
-                finish(nc.gpsimd, b - 1, 2)
-                finish(nc.gpsimd, b - 1, 3)
+                for j in range(4):
+                    finish(nc.gpsimd, b - 1, j)
 
             gate_g(b, 0)
             for j in Z_BY_UNITS:
@@ -297,9 +302,6 @@ def tile_lstmlayer_pb_t_kernel(tc, X, S, H, Uz, Ug, Wz, Wg, bz, bg, out):
             if b + 1 < BLOCKS:
                 operand_q[b + 1] = [quantise_operand(b + 1, side) for side in range(2)]
             z_times_s_by_rows(b)
-            if b > 0:
-                finish(nc.vector, b - 1, 0)
-                finish(nc.vector, b - 1, 1)
 
             gate_g(b, 1)
             if ahead < BLOCKS:

@@ -17,16 +17,14 @@ FEATURES = 512
 PACK = 4
 HALVES = 2
 WORDS = FEATURES // 2
-BLOCK_ROWS = 512
-ROW_TILES = BLOCK_ROWS // P
-BLOCKS = ROWS // BLOCK_ROWS
+TILES = [2,4,4,4,4,4,4,4,2]
+FIRST = [0,256,768,1280,1792,2304,2816,3328,3840]
+NR = [2,2,2,2,2,2,2,2,0]
+BLOCKS = len(TILES)
 UNIT_CHUNKS = FEATURES // P
 LOAD_LEAD = 3
 TRANSPOSE_LEAD = 2
 BANK_ROW_TILES = 2
-Z_BY_ROWS = range(0, 2)
-Z_BY_UNITS = range(2, 4)
-Z_COLS = 256
 GATE_Z = 0
 GATE_G = 1
 
@@ -36,33 +34,38 @@ FLOPS = 4 * 2 * ROWS * FEATURES * FEATURES
 def tile_lstmlayer_pb_t_kernel(tc, X, S, H, Uz, Ug, Wz, Wg, bz, bg, out):
     nc = tc.nc
 
-    def blocks_of(dram):
-        return dram.rearrange("(b p j) d -> b p (j d)", p=P, j=ROW_TILES)
-
-    x_blocks, s_blocks, h_blocks, out_blocks = blocks_of(X), blocks_of(S), blocks_of(H), blocks_of(out)
+    def block_of(dram, b):
+        rows = dram[FIRST[b] : FIRST[b] + TILES[b] * P, :]
+        return rows.rearrange("(p j) d -> p (j d)", p=P, j=TILES[b])
 
     with ExitStack() as ctx:
         consts = ctx.enter_context(tc.tile_pool(name="consts", bufs=1))
-        inputs = ctx.enter_context(tc.tile_pool(name="inputs", bufs=BLOCKS))
+        xin = ctx.enter_context(tc.tile_pool(name="xin", bufs=4))
+        inputs = ctx.enter_context(tc.tile_pool(name="inputs", bufs=6))
         regroup = ctx.enter_context(tc.tile_pool(name="regroup", bufs=2))
         quantised = ctx.enter_context(tc.tile_pool(name="quantised", bufs=4))
         work = ctx.enter_context(tc.tile_pool(name="work", bufs=2))
         pres = ctx.enter_context(tc.tile_pool(name="pres", bufs=2))
-        results = ctx.enter_context(tc.tile_pool(name="results", bufs=3))
+        results = ctx.enter_context(tc.tile_pool(name="results", bufs=4))
         mx_psum = ctx.enter_context(tc.psum_pool(name="mx_psum", bufs=4))
         tp_psum = ctx.enter_context(tc.psum_pool(name="tp_psum", bufs=4))
         ctx.enter_context(tc.manual_schedule())
 
         x_sb, s_sb, h_sb = {}, {}, {}
 
-        def load(dram_block, name):
-            tile_sb = inputs.tile([P, ROW_TILES * FEATURES], BF16, name=name)
-            nc.sync.dma_start(out=tile_sb[:], in_=dram_block)
+        def load(pool, dram, b, name):
+            tile_sb = pool.tile([P, TILES[b] * FEATURES], BF16, name=name)
+            nc.sync.dma_start(out=tile_sb[:], in_=block_of(dram, b))
             return tile_sb
 
-        def load_x_and_s(b):
-            x_sb[b] = load(x_blocks[b], "x_sb")
-            s_sb[b] = load(s_blocks[b], "s_sb")
+        def load_x(b):
+            x_sb[b] = load(xin, X, b, "x_sb")
+
+        def load_s(b):
+            s_sb[b] = load(inputs, S, b, "s_sb")
+
+        def load_h(b):
+            h_sb[b] = load(inputs, H, b, "h_sb")
 
         def load_weight(w, name):
             raw = consts.tile([P, PACK, FEATURES], BF16, name=name)
@@ -72,52 +75,48 @@ def tile_lstmlayer_pb_t_kernel(tc, X, S, H, Uz, Ug, Wz, Wg, bz, bg, out):
             )
             return raw
 
+        def gpsimd_copy(out, in_):
+            for h in range(1):
+                cc = slice(h * 512, (h + 1) * 512)
+                nc.gpsimd.tensor_scalar(out=out[:, cc, :], in0=in_[:, cc, :], scalar1=1.0, scalar2=0.0, op0=ALU.mult, op1=ALU.add)
+
         def regroup_weight(copy, raw):
             grouped = regroup.tile([P, FEATURES, PACK], BF16, name="w_grouped", align_bytes=64)
             copy(out=grouped[:], in_=raw[:].rearrange("p t n -> p n t"))
             return grouped
 
-        def gpsimd_copy(out, in_):
-            nc.gpsimd.tensor_scalar(out=out, in0=in_, scalar1=1.0, scalar2=0.0, op0=ALU.mult, op1=ALU.add)
-
-        def quantise(grouped_flat, pool, name):
-            codes = pool.tile([P, FEATURES], U32, name=name + "_codes", align_bytes=64)
-            scales = pool.tile([P, FEATURES], U8, name=name + "_scales", align_bytes=64)
+        def quantise(grouped_flat, n, pool, name):
+            codes = pool.tile([P, n], U32, name=name + "_codes", align_bytes=64)
+            scales = pool.tile([P, n], U8, name=name + "_scales", align_bytes=64)
             nc.vector.quantize_mx(out=codes[:].bitcast(FP8X4), scales=scales[:], in_=grouped_flat)
             return codes, scales
 
         def quantise_weight(grouped, name):
-            return quantise(grouped[:].rearrange("p n t -> p (n t)"), consts, name)
+            return quantise(grouped[:].rearrange("p n t -> p (n t)"), FEATURES, consts, name)
 
         ident = consts.tile([P, P], F32, name="ident")
         make_identity(nc, ident[:])
-
         warm = consts.tile([P, 2], F32, name="warm")
         nc.vector.memset(warm[:], 0.0)
         nc.scalar.activation(out=warm[:, 1:2], in_=warm[:, 0:1], func=TANH)
-
         bias_rows = consts.tile([P, P], BF16, name="bias_rows")
         nc.vector.memset(bias_rows[:], 0.0)
+        bz_row = consts.tile([P, FEATURES], BF16, name="bz_row")
+        nc.vector.memset(bz_row[:], 0.0)
+        ones = consts.tile([P, P], BF16, name="ones")
+        nc.vector.memset(ones[:], 1.0)
+        raw_uz = load_weight(Uz, "raw_uz")
+        load_x(0)
         for gate, bias in ((GATE_Z, bz), (GATE_G, bg)):
             nc.sync.dma_start(
                 out=bias_rows[gate * UNIT_CHUNKS : (gate + 1) * UNIT_CHUNKS, :],
                 in_=bias.rearrange("(c m) -> c m", m=P),
             )
-        bz_row = consts.tile([P, FEATURES], BF16, name="bz_row")
-        nc.vector.memset(bz_row[:], 0.0)
         nc.sync.dma_start(out=bz_row[0:1, :], in_=bz.rearrange("(o m) -> o m", o=1))
-        ones = consts.tile([P, P], BF16, name="ones")
-        nc.vector.memset(ones[:], 1.0)
-
-        raw_uz = load_weight(Uz, "raw_uz")
-        x_sb[0] = load(x_blocks[0], "x_sb")
         raw_wz = load_weight(Wz, "raw_wz")
-        s_sb[0] = load(s_blocks[0], "s_sb")
+        load_s(0)
         raw_ug = load_weight(Ug, "raw_ug")
         raw_wg = load_weight(Wg, "raw_wg")
-        for b in range(1, LOAD_LEAD):
-            load_x_and_s(b)
-            h_sb[b - 1] = load(h_blocks[b - 1], "h_sb")
 
         grouped_of = {}
         operand_q = {}
@@ -125,7 +124,6 @@ def tile_lstmlayer_pb_t_kernel(tc, X, S, H, Uz, Ug, Wz, Wg, bz, bg, out):
         tanh_z = {}
         gh_sb = {}
         z_sb = {}
-        rows_cols = slice(0, len(Z_BY_ROWS) * FEATURES)
 
         def cols_of(j):
             return slice(j * FEATURES, (j + 1) * FEATURES)
@@ -135,7 +133,7 @@ def tile_lstmlayer_pb_t_kernel(tc, X, S, H, Uz, Ug, Wz, Wg, bz, bg, out):
             words = source[:].bitcast(F32)
             if pair == 0:
                 grouped_of[b, side] = regroup.tile(
-                    [P, BLOCK_ROWS * PACK], BF16, name=("x_grouped", "s_grouped")[side], align_bytes=64
+                    [P, TILES[b] * P * PACK], BF16, name=("x_grouped", "s_grouped")[side], align_bytes=64
                 )
             grouped_words = grouped_of[b, side][:].bitcast(F32)
             bank = tp_psum.tile([P, BANK_ROW_TILES, HALVES, P], F32, name="in_bank", tag="tp")
@@ -155,7 +153,7 @@ def tile_lstmlayer_pb_t_kernel(tc, X, S, H, Uz, Ug, Wz, Wg, bz, bg, out):
             )
 
         def quantise_operand(b, side):
-            return quantise(grouped_of[b, side][:], quantised, "a")
+            return quantise(grouped_of[b, side][:], TILES[b] * P, quantised, "a")
 
         def two_passes(acc, stationary, units_or_rows, moving, columns):
             for side in range(2):
@@ -171,46 +169,46 @@ def tile_lstmlayer_pb_t_kernel(tc, X, S, H, Uz, Ug, Wz, Wg, bz, bg, out):
                     stop=(side == 1),
                 )
 
+        def by_units(gate, b, tanh_sb, columns, chunks):
+            n = columns.stop - columns.start
+            per = FEATURES // n
+            for c in range(chunks.start, chunks.stop, per):
+                m = min(per, chunks.stop - c)
+                acc = mx_psum.tile([P, m, n], F32, name="acc_units", tag="mx")
+                for i in range(m):
+                    two_passes(acc[:, i, :], weight_q[gate], slice((c + i) * P, (c + i + 1) * P), operand_q[b], columns)
+                for i in range(m):
+                    column = gate * UNIT_CHUNKS + c + i
+                    nc.scalar.activation(
+                        out=tanh_sb[:, c + i, :], in_=acc[:, i, :], func=TANH, bias=bias_col[:, column : column + 1], scale=1.0
+                    )
+
         def gate_z_by_rows(b):
-            pre = pres.tile([P, len(Z_BY_ROWS) * FEATURES], F32, name="pre")
-            z_sb[b] = results.tile([P, ROW_TILES * FEATURES], F32, name="z_sb")
-            for j in Z_BY_ROWS:
+            z_sb[b] = results.tile([P, TILES[b] * FEATURES], F32, name="z_sb")
+            if NR[b] == 0:
+                return None
+            pre = pres.tile([P, NR[b] * FEATURES], F32, name="pre")
+            for j in range(NR[b]):
                 acc = mx_psum.tile([P, FEATURES], F32, name="acc_rows", tag="mx")
                 two_passes(acc[:], operand_q[b], slice(j * P, (j + 1) * P), weight_q[GATE_Z], slice(0, FEATURES))
                 nc.vector.tensor_tensor(out=pre[:, cols_of(j)], in0=acc[:], in1=bz_full[:], op=ALU.add)
             return pre
 
         def tanh_z_by_rows(b, pre):
-            nc.scalar.activation(out=z_sb[b][:, rows_cols], in_=pre[:], func=TANH)
+            if NR[b]:
+                rc = slice(0, NR[b] * FEATURES)
+                nc.scalar.activation(out=z_sb[b][:, rc], in_=pre[:, rc], func=TANH)
 
         def gate_z_by_units(b):
-            tanh_z[b] = work.tile([P, UNIT_CHUNKS, Z_COLS], F32, name="tanh_z")
-            for c in range(UNIT_CHUNKS):
-                if c % 2 == 0:
-                    acc = mx_psum.tile([P, 2, Z_COLS], F32, name="acc_z", tag="mx")
-                columns = slice(BLOCK_ROWS - Z_COLS, BLOCK_ROWS)
-                two_passes(acc[:, c % 2, :], weight_q[GATE_Z], slice(c * P, (c + 1) * P), operand_q[b], columns)
-                if c % 2 == 1:
-                    for i in range(2):
-                        column = GATE_Z * UNIT_CHUNKS + c - 1 + i
-                        nc.scalar.activation(
-                            out=tanh_z[b][:, c - 1 + i, :],
-                            in_=acc[:, i, :],
-                            func=TANH,
-                            bias=bias_col[:, column : column + 1],
-                            scale=1.0,
-                        )
+            n = (TILES[b] - NR[b]) * P
+            if n:
+                tanh_z[b] = work.tile([P, UNIT_CHUNKS, n], F32, name="tanh_z")
+                by_units(GATE_Z, b, tanh_z[b], slice(NR[b] * P, TILES[b] * P), slice(0, UNIT_CHUNKS))
 
         def gate_g(b, part):
             if part == 0:
-                tanh_g[b] = work.tile([P, UNIT_CHUNKS, BLOCK_ROWS], F32, name="tanh_g")
-            for c in range(2 * part, 2 * part + 2):
-                acc = mx_psum.tile([P, BLOCK_ROWS], F32, name="acc_g", tag="mx")
-                two_passes(acc[:], weight_q[GATE_G], slice(c * P, (c + 1) * P), operand_q[b], slice(0, BLOCK_ROWS))
-                column = GATE_G * UNIT_CHUNKS + c
-                nc.scalar.activation(
-                    out=tanh_g[b][:, c, :], in_=acc[:], func=TANH, bias=bias_col[:, column : column + 1], scale=1.0
-                )
+                tanh_g[b] = work.tile([P, UNIT_CHUNKS, TILES[b] * P], F32, name="tanh_g")
+            by_units(GATE_G, b, tanh_g[b], slice(0, TILES[b] * P), slice(2 * part, 2 * part + 2))
 
         def transpose_back(source, first):
             bank = tp_psum.tile([P, FEATURES], F32, name="back_bank", tag="tp")
@@ -221,17 +219,17 @@ def tile_lstmlayer_pb_t_kernel(tc, X, S, H, Uz, Ug, Wz, Wg, bz, bg, out):
             return bank
 
         def z_times_s_by_units(b, j):
-            bank = transpose_back(tanh_z[b], (j - Z_BY_UNITS.start) * P)
+            bank = transpose_back(tanh_z[b], (j - NR[b]) * P)
             nc.vector.tensor_tensor(out=z_sb[b][:, cols_of(j)], in0=bank[:], in1=s_sb[b][:, cols_of(j)], op=ALU.mult)
 
         def z_times_s_by_rows(b):
-            nc.vector.tensor_tensor(
-                out=z_sb[b][:, rows_cols], in0=z_sb[b][:, rows_cols], in1=s_sb[b][:, rows_cols], op=ALU.mult
-            )
+            if NR[b]:
+                rc = slice(0, NR[b] * FEATURES)
+                nc.vector.tensor_tensor(out=z_sb[b][:, rc], in0=z_sb[b][:, rc], in1=s_sb[b][:, rc], op=ALU.mult)
 
         def g_times_h(b, j):
             if j == 0:
-                gh_sb[b] = work.tile([P, ROW_TILES * FEATURES], F32, name="gh_sb")
+                gh_sb[b] = work.tile([P, TILES[b] * FEATURES], F32, name="gh_sb")
             bank = transpose_back(tanh_g[b], j * P)
             nc.vector.scalar_tensor_tensor(
                 out=gh_sb[b][:, cols_of(j)],
@@ -245,8 +243,15 @@ def tile_lstmlayer_pb_t_kernel(tc, X, S, H, Uz, Ug, Wz, Wg, bz, bg, out):
         def finish(engine, b, j):
             cols = cols_of(j)
             engine.tensor_tensor(out=z_sb[b][:, cols], in0=z_sb[b][:, cols], in1=gh_sb[b][:, cols], op=ALU.subtract)
-            nc.sync.dma_start(out=out_blocks[b][:, cols], in_=z_sb[b][:, cols])
+            nc.sync.dma_start(out=block_of(out, b)[:, cols], in_=z_sb[b][:, cols])
 
+        def warm_up(count):
+            warm_bank = mx_psum.tile([P, FEATURES], F32, name="warm_bank", tag="mx")
+            for i in range(count):
+                nc.tensor.matmul(out=warm_bank[:], lhsT=ones[:], rhs=bz_row[:], start=True, stop=True)
+
+        for pair in range(TILES[0] // 2):
+            transpose_operand(0, 0, pair)
         bias_rows_f32 = consts.tile([P, P], F32, name="bias_rows_f32")
         nc.scalar.copy(out=bias_rows_f32[:], in_=bias_rows[:])
         bias_bank = tp_psum.tile([P, P], F32, name="bias_bank", tag="tp")
@@ -257,10 +262,7 @@ def tile_lstmlayer_pb_t_kernel(tc, X, S, H, Uz, Ug, Wz, Wg, bz, bg, out):
         nc.tensor.matmul(out=bz_bank[:], lhsT=ones[:], rhs=bz_row[:], start=True, stop=True)
         bz_full = consts.tile([P, FEATURES], F32, name="bz_full")
         nc.scalar.copy(out=bz_full[:], in_=bz_bank[:])
-
-        for pair in range(2):
-            transpose_operand(0, 0, pair)
-        for pair in range(2):
+        for pair in range(TILES[0] // 2):
             transpose_operand(0, 1, pair)
         grouped_uz = regroup_weight(nc.vector.tensor_copy, raw_uz)
         uz_q = quantise_weight(grouped_uz, "uz")
@@ -268,17 +270,26 @@ def tile_lstmlayer_pb_t_kernel(tc, X, S, H, Uz, Ug, Wz, Wg, bz, bg, out):
         x0_q = quantise_operand(0, 0)
         wz_q = quantise_weight(grouped_wz, "wz")
         s0_q = quantise_operand(0, 1)
-        grouped_ug = regroup_weight(gpsimd_copy, raw_ug)
-        grouped_wg = regroup_weight(gpsimd_copy, raw_wg)
+        grouped_ug = regroup_weight(nc.scalar.copy, raw_ug)
+        grouped_wg = regroup_weight(nc.vector.tensor_copy, raw_wg)
         operand_q[0] = [x0_q, s0_q]
         weight_q = {GATE_Z: [uz_q, wz_q]}
+        last = BLOCKS - 1
+        for b in range(1, LOAD_LEAD):
+            if b not in x_sb:
+                load_x(b)
+            if b not in s_sb:
+                load_s(b)
+            load_h(b - 1)
 
         for b in range(BLOCKS):
             if b + LOAD_LEAD < BLOCKS:
-                load_x_and_s(b + LOAD_LEAD)
+                load_x(b + LOAD_LEAD)
+                load_s(b + LOAD_LEAD)
             if b + LOAD_LEAD - 1 < BLOCKS:
-                h_sb[b + LOAD_LEAD - 1] = load(h_blocks[b + LOAD_LEAD - 1], "h_sb")
+                load_h(b + LOAD_LEAD - 1)
             ahead = b + TRANSPOSE_LEAD
+            ahead_pairs = [(side, pair) for side in range(2) for pair in range(TILES[ahead] // 2)] if ahead < BLOCKS else []
 
             pre = gate_z_by_rows(b)
             gate_z_by_units(b)
@@ -286,32 +297,36 @@ def tile_lstmlayer_pb_t_kernel(tc, X, S, H, Uz, Ug, Wz, Wg, bz, bg, out):
             if b == 0:
                 weight_q[GATE_G] = [quantise_weight(grouped_ug, "ug"), quantise_weight(grouped_wg, "wg")]
                 for side in range(2):
-                    for pair in range(2):
+                    for pair in range(TILES[1] // 2):
                         transpose_operand(1, side, pair)
             else:
-                for j in range(ROW_TILES):
+                for j in range(TILES[b - 1]):
                     g_times_h(b - 1, j)
-                for j in range(4):
-                    finish(nc.gpsimd, b - 1, j)
 
             gate_g(b, 0)
-            for j in Z_BY_UNITS:
+            for j in range(NR[b], TILES[b]):
                 z_times_s_by_units(b, j)
-            if ahead < BLOCKS:
-                transpose_operand(ahead, 0, 0)
+            for side, pair in ahead_pairs[:1]:
+                transpose_operand(ahead, side, pair)
             if b + 1 < BLOCKS:
                 operand_q[b + 1] = [quantise_operand(b + 1, side) for side in range(2)]
-            z_times_s_by_rows(b)
+            if 0 < b < last:
+                z_times_s_by_rows(b - 1)
+                for j in range(TILES[b - 1]):
+                    finish(nc.gpsimd, b - 1, j)
+            if b == last:
+                z_times_s_by_rows(b - 1)
+                for j in range(0, 2):
+                    finish(nc.gpsimd, b - 1, j)
 
             gate_g(b, 1)
-            if ahead < BLOCKS:
-                transpose_operand(ahead, 0, 1)
-                for pair in range(2):
-                    transpose_operand(ahead, 1, pair)
+            for side, pair in ahead_pairs[1:]:
+                transpose_operand(ahead, side, pair)
 
-        last = BLOCKS - 1
-        for j in range(0, ROW_TILES, 2):
+        z_times_s_by_rows(last)
+        for j in range(TILES[last]):
             g_times_h(last, j)
-            g_times_h(last, j + 1)
-            finish(nc.gpsimd, last, j)
-            finish(nc.vector, last, j + 1)
+        for j in range(TILES[last]):
+            finish(nc.vector, last - 1, j + 2)
+        for j in range(TILES[last]):
+            finish(nc.vector, last, j)

@@ -19,7 +19,7 @@ HALVES = 2
 WORDS = FEATURES // 2
 TILES = [2,4,4,4,4,4,4,4,2]
 FIRST = [0,256,768,1280,1792,2304,2816,3328,3840]
-NR = [2,2,2,2,2,2,2,2,0]
+NR = [2,3,3,3,3,3,3,2,0]
 BLOCKS = len(TILES)
 UNIT_CHUNKS = FEATURES // P
 LOAD_LEAD = 3
@@ -82,7 +82,10 @@ def tile_lstmlayer_pb_t_kernel(tc, X, S, H, Uz, Ug, Wz, Wg, bz, bg, out):
 
         def regroup_weight(copy, raw):
             grouped = regroup.tile([P, FEATURES, PACK], BF16, name="w_grouped", align_bytes=64)
-            copy(out=grouped[:], in_=raw[:].rearrange("p t n -> p n t"))
+            copy(
+                out=grouped[:].rearrange("p (c i) t -> p c t i", i=4),
+                in_=raw[:].rearrange("p t (c i) -> p c t i", i=4),
+            )
             return grouped
 
         def quantise(grouped_flat, n, pool, name):
@@ -99,12 +102,12 @@ def tile_lstmlayer_pb_t_kernel(tc, X, S, H, Uz, Ug, Wz, Wg, bz, bg, out):
         warm = consts.tile([P, 2], F32, name="warm")
         nc.vector.memset(warm[:], 0.0)
         nc.scalar.activation(out=warm[:, 1:2], in_=warm[:, 0:1], func=TANH)
+        ones = consts.tile([P, FEATURES], BF16, name="ones")
+        nc.vector.memset(ones[:], 1.0)
         bias_rows = consts.tile([P, P], BF16, name="bias_rows")
         nc.vector.memset(bias_rows[:], 0.0)
         bz_row = consts.tile([P, FEATURES], BF16, name="bz_row")
         nc.vector.memset(bz_row[:], 0.0)
-        ones = consts.tile([P, P], BF16, name="ones")
-        nc.vector.memset(ones[:], 1.0)
         raw_uz = load_weight(Uz, "raw_uz")
         load_x(0)
         for gate, bias in ((GATE_Z, bz), (GATE_G, bg)):
@@ -248,8 +251,9 @@ def tile_lstmlayer_pb_t_kernel(tc, X, S, H, Uz, Ug, Wz, Wg, bz, bg, out):
         def warm_up(count):
             warm_bank = mx_psum.tile([P, FEATURES], F32, name="warm_bank", tag="mx")
             for i in range(count):
-                nc.tensor.matmul(out=warm_bank[:], lhsT=ones[:], rhs=bz_row[:], start=True, stop=True)
+                nc.tensor.matmul(out=warm_bank[:], lhsT=ones[:, 0:P], rhs=ones[:], start=True, stop=True)
 
+        warm_up(5)
         for pair in range(TILES[0] // 2):
             transpose_operand(0, 0, pair)
         bias_rows_f32 = consts.tile([P, P], F32, name="bias_rows_f32")
@@ -259,11 +263,13 @@ def tile_lstmlayer_pb_t_kernel(tc, X, S, H, Uz, Ug, Wz, Wg, bz, bg, out):
         bias_col = consts.tile([P, 2 * UNIT_CHUNKS], F32, name="bias_col")
         nc.scalar.copy(out=bias_col[:], in_=bias_bank[:, 0 : 2 * UNIT_CHUNKS])
         bz_bank = tp_psum.tile([P, FEATURES], F32, name="bz_bank", tag="tp")
-        nc.tensor.matmul(out=bz_bank[:], lhsT=ones[:], rhs=bz_row[:], start=True, stop=True)
+        nc.tensor.matmul(out=bz_bank[:], lhsT=ones[:, 0:P], rhs=bz_row[:], start=True, stop=True)
         bz_full = consts.tile([P, FEATURES], F32, name="bz_full")
         nc.scalar.copy(out=bz_full[:], in_=bz_bank[:])
+        warm_up(1)
         for pair in range(TILES[0] // 2):
             transpose_operand(0, 1, pair)
+        warm_up(1)
         grouped_uz = regroup_weight(nc.vector.tensor_copy, raw_uz)
         uz_q = quantise_weight(grouped_uz, "uz")
         grouped_wz = regroup_weight(nc.vector.tensor_copy, raw_wz)
@@ -291,16 +297,23 @@ def tile_lstmlayer_pb_t_kernel(tc, X, S, H, Uz, Ug, Wz, Wg, bz, bg, out):
             ahead = b + TRANSPOSE_LEAD
             ahead_pairs = [(side, pair) for side in range(2) for pair in range(TILES[ahead] // 2)] if ahead < BLOCKS else []
 
+            half = TILES[b - 1] // 2
+            first_pairs = [(side, pair) for side in range(2) for pair in range(TILES[1] // 2)]
             pre = gate_z_by_rows(b)
+            if b == 0:
+                for side, pair in first_pairs[:2]:
+                    transpose_operand(1, side, pair)
+            else:
+                for j in range(half):
+                    g_times_h(b - 1, j)
             gate_z_by_units(b)
             tanh_z_by_rows(b, pre)
             if b == 0:
                 weight_q[GATE_G] = [quantise_weight(grouped_ug, "ug"), quantise_weight(grouped_wg, "wg")]
-                for side in range(2):
-                    for pair in range(TILES[1] // 2):
-                        transpose_operand(1, side, pair)
+                for side, pair in first_pairs[2:]:
+                    transpose_operand(1, side, pair)
             else:
-                for j in range(TILES[b - 1]):
+                for j in range(half, TILES[b - 1]):
                     g_times_h(b - 1, j)
 
             gate_g(b, 0)

@@ -20,6 +20,8 @@ WORDS = FEATURES // 2
 TILES = [2,4,4,4,4,4,4,4,2]
 FIRST = [0,256,768,1280,1792,2304,2816,3328,3840]
 NR = [2,3,3,3,3,3,3,2,0]
+EARLY = [7]
+GSUBS = {7:2}
 BLOCKS = len(TILES)
 UNIT_CHUNKS = FEATURES // P
 LOAD_LEAD = 3
@@ -101,21 +103,18 @@ def tile_lstmlayer_pb_t_kernel(tc, X, S, H, Uz, Ug, Wz, Wg, bz, bg, out):
         make_identity(nc, ident[:])
         warm = consts.tile([P, 2], F32, name="warm")
         nc.vector.memset(warm[:], 0.0)
-        nc.scalar.activation(out=warm[:, 1:2], in_=warm[:, 0:1], func=TANH)
-        ones = consts.tile([P, FEATURES], BF16, name="ones")
-        nc.vector.memset(ones[:], 1.0)
         bias_rows = consts.tile([P, P], BF16, name="bias_rows")
         nc.vector.memset(bias_rows[:], 0.0)
-        bz_row = consts.tile([P, FEATURES], BF16, name="bz_row")
-        nc.vector.memset(bz_row[:], 0.0)
-        raw_uz = load_weight(Uz, "raw_uz")
-        load_x(0)
         for gate, bias in ((GATE_Z, bz), (GATE_G, bg)):
             nc.sync.dma_start(
                 out=bias_rows[gate * UNIT_CHUNKS : (gate + 1) * UNIT_CHUNKS, :],
                 in_=bias.rearrange("(c m) -> c m", m=P),
             )
-        nc.sync.dma_start(out=bz_row[0:1, :], in_=bz.rearrange("(o m) -> o m", o=1))
+        ones = consts.tile([P, FEATURES], BF16, name="ones")
+        nc.vector.memset(ones[:], 1.0)
+        nc.scalar.activation(out=warm[:, 1:2], in_=warm[:, 0:1], func=TANH)
+        raw_uz = load_weight(Uz, "raw_uz")
+        load_x(0)
         raw_wz = load_weight(Wz, "raw_wz")
         load_s(0)
         raw_ug = load_weight(Ug, "raw_ug")
@@ -253,9 +252,7 @@ def tile_lstmlayer_pb_t_kernel(tc, X, S, H, Uz, Ug, Wz, Wg, bz, bg, out):
             for i in range(count):
                 nc.tensor.matmul(out=warm_bank[:], lhsT=ones[:, 0:P], rhs=ones[:], start=True, stop=True)
 
-        warm_up(5)
-        for pair in range(TILES[0] // 2):
-            transpose_operand(0, 0, pair)
+        warm_up(3)
         bias_rows_f32 = consts.tile([P, P], F32, name="bias_rows_f32")
         nc.scalar.copy(out=bias_rows_f32[:], in_=bias_rows[:])
         bias_bank = tp_psum.tile([P, P], F32, name="bias_bank", tag="tp")
@@ -263,13 +260,20 @@ def tile_lstmlayer_pb_t_kernel(tc, X, S, H, Uz, Ug, Wz, Wg, bz, bg, out):
         bias_col = consts.tile([P, 2 * UNIT_CHUNKS], F32, name="bias_col")
         nc.scalar.copy(out=bias_col[:], in_=bias_bank[:, 0 : 2 * UNIT_CHUNKS])
         bz_bank = tp_psum.tile([P, FEATURES], F32, name="bz_bank", tag="tp")
-        nc.tensor.matmul(out=bz_bank[:], lhsT=ones[:, 0:P], rhs=bz_row[:], start=True, stop=True)
+        for c in range(UNIT_CHUNKS):
+            nc.tensor.matmul(
+                out=bz_bank[:, c * P : (c + 1) * P],
+                lhsT=ident[:, c : c + 1].to_broadcast([P, P]),
+                rhs=bias_rows_f32[:],
+                start=True,
+                stop=True,
+            )
         bz_full = consts.tile([P, FEATURES], F32, name="bz_full")
         nc.scalar.copy(out=bz_full[:], in_=bz_bank[:])
-        warm_up(1)
+        for pair in range(TILES[0] // 2):
+            transpose_operand(0, 0, pair)
         for pair in range(TILES[0] // 2):
             transpose_operand(0, 1, pair)
-        warm_up(1)
         grouped_uz = regroup_weight(nc.vector.tensor_copy, raw_uz)
         uz_q = quantise_weight(grouped_uz, "uz")
         grouped_wz = regroup_weight(nc.vector.tensor_copy, raw_wz)
@@ -297,49 +301,45 @@ def tile_lstmlayer_pb_t_kernel(tc, X, S, H, Uz, Ug, Wz, Wg, bz, bg, out):
             ahead = b + TRANSPOSE_LEAD
             ahead_pairs = [(side, pair) for side in range(2) for pair in range(TILES[ahead] // 2)] if ahead < BLOCKS else []
 
-            half = TILES[b - 1] // 2
             first_pairs = [(side, pair) for side in range(2) for pair in range(TILES[1] // 2)]
+            back_first = min(3, TILES[b - 1])
             pre = gate_z_by_rows(b)
-            if b == 0:
-                for side, pair in first_pairs[:2]:
-                    transpose_operand(1, side, pair)
-            else:
-                for j in range(half):
-                    g_times_h(b - 1, j)
             gate_z_by_units(b)
-            tanh_z_by_rows(b, pre)
             if b == 0:
                 weight_q[GATE_G] = [quantise_weight(grouped_ug, "ug"), quantise_weight(grouped_wg, "wg")]
-                for side, pair in first_pairs[2:]:
+                for side, pair in first_pairs:
                     transpose_operand(1, side, pair)
-            else:
-                for j in range(half, TILES[b - 1]):
+            tanh_z_by_rows(b, pre)
+            if b > 0:
+                for j in range(back_first):
                     g_times_h(b - 1, j)
-
             gate_g(b, 0)
+            if b == 0:
+                pass
+            else:
+                for j in range(back_first, TILES[b - 1]):
+                    g_times_h(b - 1, j)
             for j in range(NR[b], TILES[b]):
                 z_times_s_by_units(b, j)
             for side, pair in ahead_pairs[:1]:
                 transpose_operand(ahead, side, pair)
             if b + 1 < BLOCKS:
                 operand_q[b + 1] = [quantise_operand(b + 1, side) for side in range(2)]
-            if 0 < b < last:
+            if 0 < b and b - 1 not in EARLY:
                 z_times_s_by_rows(b - 1)
+            if b in EARLY:
+                z_times_s_by_rows(b)
+            if 0 < b:
                 for j in range(TILES[b - 1]):
-                    finish(nc.gpsimd, b - 1, j)
-            if b == last:
-                z_times_s_by_rows(b - 1)
-                for j in range(0, 2):
-                    finish(nc.gpsimd, b - 1, j)
-
+                    if j < GSUBS.get(b - 1, 4):
+                        finish(nc.gpsimd, b - 1, j)
             gate_g(b, 1)
             for side, pair in ahead_pairs[1:]:
                 transpose_operand(ahead, side, pair)
 
-        z_times_s_by_rows(last)
         for j in range(TILES[last]):
             g_times_h(last, j)
-        for j in range(TILES[last]):
-            finish(nc.vector, last - 1, j + 2)
+        for j in range(GSUBS.get(last - 1, 4), TILES[last - 1]):
+            finish(nc.vector, last - 1, j)
         for j in range(TILES[last]):
             finish(nc.vector, last, j)

@@ -22,6 +22,8 @@ FIRST = [0,256,768,1280,1792,2304,2816,3328,3840]
 NR = [2,3,3,3,3,3,3,2,0]
 EARLY = [7]
 GSUBS = {7:2}
+VSET = [(1,1,0),(1,1,1)]
+GMERGE = [1,2,3,4,5,6]
 BLOCKS = len(TILES)
 UNIT_CHUNKS = FEATURES // P
 LOAD_LEAD = 3
@@ -147,7 +149,8 @@ def tile_lstmlayer_pb_t_kernel(tc, X, S, H, Uz, Ug, Wz, Wg, bz, bg, out):
                         in_=words[:, first + u * P : first + (u + 1) * P],
                         identity=ident[:],
                     )
-            nc.scalar.copy(
+            copy = nc.vector.tensor_copy if (b, side, pair) in VSET else nc.scalar.copy
+            copy(
                 out=grouped_words[:, pair * BANK_ROW_TILES * WORDS : (pair + 1) * BANK_ROW_TILES * WORDS].rearrange(
                     "p (i r u) -> p i r u", i=BANK_ROW_TILES, u=HALVES
                 ),
@@ -225,8 +228,9 @@ def tile_lstmlayer_pb_t_kernel(tc, X, S, H, Uz, Ug, Wz, Wg, bz, bg, out):
             nc.vector.tensor_tensor(out=z_sb[b][:, cols_of(j)], in0=bank[:], in1=s_sb[b][:, cols_of(j)], op=ALU.mult)
 
         def z_times_s_by_rows(b):
-            if NR[b]:
-                rc = slice(0, NR[b] * FEATURES)
+            n = NR[b]
+            if n:
+                rc = slice(0, n * FEATURES)
                 nc.vector.tensor_tensor(out=z_sb[b][:, rc], in0=z_sb[b][:, rc], in1=s_sb[b][:, rc], op=ALU.mult)
 
         def g_times_h(b, j):
@@ -241,6 +245,14 @@ def tile_lstmlayer_pb_t_kernel(tc, X, S, H, Uz, Ug, Wz, Wg, bz, bg, out):
                 op0=ALU.subtract,
                 op1=ALU.mult,
             )
+
+        def finish_block(b):
+            n = GSUBS.get(b, 4)
+            cols = slice(0, n * FEATURES)
+            nc.gpsimd.tensor_tensor(out=z_sb[b][:, cols], in0=z_sb[b][:, cols], in1=gh_sb[b][:, cols], op=ALU.subtract)
+            for s in range(n // 2):
+                cols = slice(2 * s * FEATURES, 2 * (s + 1) * FEATURES)
+                nc.sync.dma_start(out=block_of(out, b)[:, cols], in_=z_sb[b][:, cols])
 
         def finish(engine, b, j):
             cols = cols_of(j)
@@ -329,7 +341,9 @@ def tile_lstmlayer_pb_t_kernel(tc, X, S, H, Uz, Ug, Wz, Wg, bz, bg, out):
                 z_times_s_by_rows(b - 1)
             if b in EARLY:
                 z_times_s_by_rows(b)
-            if 0 < b:
+            if b - 1 in GMERGE:
+                finish_block(b - 1)
+            elif 0 < b:
                 for j in range(TILES[b - 1]):
                     if j < GSUBS.get(b - 1, 4):
                         finish(nc.gpsimd, b - 1, j)

@@ -19,11 +19,11 @@ HALVES = 2
 WORDS = FEATURES // 2
 TILES = [2,4,4,4,4,4,4,4,2]
 FIRST = [0,256,768,1280,1792,2304,2816,3328,3840]
-NR = [2,3,3,3,3,3,3,2,0]
+NR = [2,3,3,3,3,3,2,2,0]
 EARLY = [7]
-GSUBS = {7:2}
+GSUBS = {7:1}
 VSET = [(1,1,0),(1,1,1)]
-GMERGE = [1,2,3,4,5,6]
+GMERGE = [1,2,3,4,5]
 BLOCKS = len(TILES)
 UNIT_CHUNKS = FEATURES // P
 LOAD_LEAD = 3

from contextlib import ExitStack

import concourse.mybir as mybir
from concourse.masks import make_identity

F32 = mybir.dt.float32
BF16 = mybir.dt.bfloat16
U32 = mybir.dt.uint32
U8 = mybir.dt.uint8
FP8X4 = mybir.dt.float8_e4m3fn_x4
ALU = mybir.AluOpType
TANH = mybir.ActivationFunctionType.Tanh

P = 128
ROWS = 4096
FEATURES = 512
PACK = 4
HALVES = 2
WORDS = FEATURES // 2
TILES = [2,4,4,4,4,4,4,4,2]
FIRST = [0,256,768,1280,1792,2304,2816,3328,3840]
NR = [2,3,3,3,3,3,2,2,0]
EARLY = [7]
GSUBS = {7:1}
VSET = [(1,1,0),(1,1,1)]
GMERGE = [1,2,3,4,5]
BLOCKS = len(TILES)
UNIT_CHUNKS = FEATURES // P
LOAD_LEAD = 3
TRANSPOSE_LEAD = 2
BANK_ROW_TILES = 2
GATE_Z = 0
GATE_G = 1

FLOPS = 4 * 2 * ROWS * FEATURES * FEATURES


def tile_lstmlayer_pb_t_kernel(tc, X, S, H, Uz, Ug, Wz, Wg, bz, bg, out):
    nc = tc.nc

    def block_of(dram, b):
        rows = dram[FIRST[b] : FIRST[b] + TILES[b] * P, :]
        return rows.rearrange("(p j) d -> p (j d)", p=P, j=TILES[b])

    with ExitStack() as ctx:
        consts = ctx.enter_context(tc.tile_pool(name="consts", bufs=1))
        xin = ctx.enter_context(tc.tile_pool(name="xin", bufs=4))
        inputs = ctx.enter_context(tc.tile_pool(name="inputs", bufs=6))
        regroup = ctx.enter_context(tc.tile_pool(name="regroup", bufs=2))
        quantised = ctx.enter_context(tc.tile_pool(name="quantised", bufs=4))
        work = ctx.enter_context(tc.tile_pool(name="work", bufs=2))
        pres = ctx.enter_context(tc.tile_pool(name="pres", bufs=2))
        results = ctx.enter_context(tc.tile_pool(name="results", bufs=4))
        mx_psum = ctx.enter_context(tc.psum_pool(name="mx_psum", bufs=4))
        tp_psum = ctx.enter_context(tc.psum_pool(name="tp_psum", bufs=4))
        ctx.enter_context(tc.manual_schedule())

        x_sb, s_sb, h_sb = {}, {}, {}

        def load(pool, dram, b, name):
            tile_sb = pool.tile([P, TILES[b] * FEATURES], BF16, name=name)
            nc.sync.dma_start(out=tile_sb[:], in_=block_of(dram, b))
            return tile_sb

        def load_x(b):
            x_sb[b] = load(xin, X, b, "x_sb")

        def load_s(b):
            s_sb[b] = load(inputs, S, b, "s_sb")

        def load_h(b):
            h_sb[b] = load(inputs, H, b, "h_sb")

        def load_weight(w, name):
            raw = consts.tile([P, PACK, FEATURES], BF16, name=name)
            nc.sync.dma_start(
                out=raw[:].rearrange("p (u e) n -> p u e n", e=2),
                in_=w.rearrange("(u p e) n -> p u e n", u=HALVES, e=2),
            )
            return raw

        def gpsimd_copy(out, in_):
            for h in range(1):
                cc = slice(h * 512, (h + 1) * 512)
                nc.gpsimd.tensor_scalar(out=out[:, cc, :], in0=in_[:, cc, :], scalar1=1.0, scalar2=0.0, op0=ALU.mult, op1=ALU.add)

        def regroup_weight(copy, raw):
            grouped = regroup.tile([P, FEATURES, PACK], BF16, name="w_grouped", align_bytes=64)
            copy(
                out=grouped[:].rearrange("p (c i) t -> p c t i", i=4),
                in_=raw[:].rearrange("p t (c i) -> p c t i", i=4),
            )
            return grouped

        def quantise(grouped_flat, n, pool, name):
            codes = pool.tile([P, n], U32, name=name + "_codes", align_bytes=64)
            scales = pool.tile([P, n], U8, name=name + "_scales", align_bytes=64)
            nc.vector.quantize_mx(out=codes[:].bitcast(FP8X4), scales=scales[:], in_=grouped_flat)
            return codes, scales

        def quantise_weight(grouped, name):
            return quantise(grouped[:].rearrange("p n t -> p (n t)"), FEATURES, consts, name)

        ident = consts.tile([P, P], F32, name="ident")
        make_identity(nc, ident[:])
        warm = consts.tile([P, 2], F32, name="warm")
        nc.vector.memset(warm[:], 0.0)
        bias_rows = consts.tile([P, P], BF16, name="bias_rows")
        nc.vector.memset(bias_rows[:], 0.0)
        for gate, bias in ((GATE_Z, bz), (GATE_G, bg)):
            nc.sync.dma_start(
                out=bias_rows[gate * UNIT_CHUNKS : (gate + 1) * UNIT_CHUNKS, :],
                in_=bias.rearrange("(c m) -> c m", m=P),
            )
        ones = consts.tile([P, FEATURES], BF16, name="ones")
        nc.vector.memset(ones[:], 1.0)
        nc.scalar.activation(out=warm[:, 1:2], in_=warm[:, 0:1], func=TANH)
        raw_uz = load_weight(Uz, "raw_uz")
        load_x(0)
        raw_wz = load_weight(Wz, "raw_wz")
        load_s(0)
        raw_ug = load_weight(Ug, "raw_ug")
        raw_wg = load_weight(Wg, "raw_wg")

        grouped_of = {}
        operand_q = {}
        tanh_g = {}
        tanh_z = {}
        gh_sb = {}
        z_sb = {}

        def cols_of(j):
            return slice(j * FEATURES, (j + 1) * FEATURES)

        def transpose_operand(b, side, pair):
            source = (x_sb, s_sb)[side][b]
            words = source[:].bitcast(F32)
            if pair == 0:
                grouped_of[b, side] = regroup.tile(
                    [P, TILES[b] * P * PACK], BF16, name=("x_grouped", "s_grouped")[side], align_bytes=64
                )
            grouped_words = grouped_of[b, side][:].bitcast(F32)
            bank = tp_psum.tile([P, BANK_ROW_TILES, HALVES, P], F32, name="in_bank", tag="tp")
            for i in range(BANK_ROW_TILES):
                first = (BANK_ROW_TILES * pair + i) * WORDS
                for u in range(HALVES):
                    nc.tensor.transpose(
                        out=bank[:, i, u, :],
                        in_=words[:, first + u * P : first + (u + 1) * P],
                        identity=ident[:],
                    )
            copy = nc.vector.tensor_copy if (b, side, pair) in VSET else nc.scalar.copy
            copy(
                out=grouped_words[:, pair * BANK_ROW_TILES * WORDS : (pair + 1) * BANK_ROW_TILES * WORDS].rearrange(
                    "p (i r u) -> p i r u", i=BANK_ROW_TILES, u=HALVES
                ),
                in_=bank[:].rearrange("p i u r -> p i r u"),
            )

        def quantise_operand(b, side):
            return quantise(grouped_of[b, side][:], TILES[b] * P, quantised, "a")

        def two_passes(acc, stationary, units_or_rows, moving, columns):
            for side in range(2):
                l_codes, l_scales = stationary[side]
                r_codes, r_scales = moving[side]
                nc.tensor.matmul_mx(
                    out=acc,
                    lhsT=l_codes[:, units_or_rows].bitcast(FP8X4),
                    lhsT_scale=l_scales[:, units_or_rows],
                    rhs=r_codes[:, columns].bitcast(FP8X4),
                    rhs_scale=r_scales[:, columns],
                    start=(side == 0),
                    stop=(side == 1),
                )

        def by_units(gate, b, tanh_sb, columns, chunks):
            n = columns.stop - columns.start
            per = FEATURES // n
            for c in range(chunks.start, chunks.stop, per):
                m = min(per, chunks.stop - c)
                acc = mx_psum.tile([P, m, n], F32, name="acc_units", tag="mx")
                for i in range(m):
                    two_passes(acc[:, i, :], weight_q[gate], slice((c + i) * P, (c + i + 1) * P), operand_q[b], columns)
                for i in range(m):
                    column = gate * UNIT_CHUNKS + c + i
                    nc.scalar.activation(
                        out=tanh_sb[:, c + i, :], in_=acc[:, i, :], func=TANH, bias=bias_col[:, column : column + 1], scale=1.0
                    )

        def gate_z_by_rows(b):
            z_sb[b] = results.tile([P, TILES[b] * FEATURES], F32, name="z_sb")
            if NR[b] == 0:
                return None
            pre = pres.tile([P, NR[b] * FEATURES], F32, name="pre")
            for j in range(NR[b]):
                acc = mx_psum.tile([P, FEATURES], F32, name="acc_rows", tag="mx")
                two_passes(acc[:], operand_q[b], slice(j * P, (j + 1) * P), weight_q[GATE_Z], slice(0, FEATURES))
                nc.vector.tensor_tensor(out=pre[:, cols_of(j)], in0=acc[:], in1=bz_full[:], op=ALU.add)
            return pre

        def tanh_z_by_rows(b, pre):
            if NR[b]:
                rc = slice(0, NR[b] * FEATURES)
                nc.scalar.activation(out=z_sb[b][:, rc], in_=pre[:, rc], func=TANH)

        def gate_z_by_units(b):
            n = (TILES[b] - NR[b]) * P
            if n:
                tanh_z[b] = work.tile([P, UNIT_CHUNKS, n], F32, name="tanh_z")
                by_units(GATE_Z, b, tanh_z[b], slice(NR[b] * P, TILES[b] * P), slice(0, UNIT_CHUNKS))

        def gate_g(b, part):
            if part == 0:
                tanh_g[b] = work.tile([P, UNIT_CHUNKS, TILES[b] * P], F32, name="tanh_g")
            by_units(GATE_G, b, tanh_g[b], slice(0, TILES[b] * P), slice(2 * part, 2 * part + 2))

        def transpose_back(source, first):
            bank = tp_psum.tile([P, FEATURES], F32, name="back_bank", tag="tp")
            for c in range(UNIT_CHUNKS):
                nc.tensor.transpose(
                    out=bank[:, c * P : (c + 1) * P], in_=source[:, c, first : first + P], identity=ident[:]
                )
            return bank

        def z_times_s_by_units(b, j):
            bank = transpose_back(tanh_z[b], (j - NR[b]) * P)
            nc.vector.tensor_tensor(out=z_sb[b][:, cols_of(j)], in0=bank[:], in1=s_sb[b][:, cols_of(j)], op=ALU.mult)

        def z_times_s_by_rows(b):
            n = NR[b]
            if n:
                rc = slice(0, n * FEATURES)
                nc.vector.tensor_tensor(out=z_sb[b][:, rc], in0=z_sb[b][:, rc], in1=s_sb[b][:, rc], op=ALU.mult)

        def g_times_h(b, j):
            if j == 0:
                gh_sb[b] = work.tile([P, TILES[b] * FEATURES], F32, name="gh_sb")
            bank = transpose_back(tanh_g[b], j * P)
            nc.vector.scalar_tensor_tensor(
                out=gh_sb[b][:, cols_of(j)],
                in0=bank[:],
                scalar=1.0,
                in1=h_sb[b][:, cols_of(j)],
                op0=ALU.subtract,
                op1=ALU.mult,
            )

        def finish_block(b):
            n = GSUBS.get(b, 4)
            cols = slice(0, n * FEATURES)
            nc.gpsimd.tensor_tensor(out=z_sb[b][:, cols], in0=z_sb[b][:, cols], in1=gh_sb[b][:, cols], op=ALU.subtract)
            for s in range(n // 2):
                cols = slice(2 * s * FEATURES, 2 * (s + 1) * FEATURES)
                nc.sync.dma_start(out=block_of(out, b)[:, cols], in_=z_sb[b][:, cols])

        def finish(engine, b, j):
            cols = cols_of(j)
            engine.tensor_tensor(out=z_sb[b][:, cols], in0=z_sb[b][:, cols], in1=gh_sb[b][:, cols], op=ALU.subtract)
            nc.sync.dma_start(out=block_of(out, b)[:, cols], in_=z_sb[b][:, cols])

        def warm_up(count):
            warm_bank = mx_psum.tile([P, FEATURES], F32, name="warm_bank", tag="mx")
            for i in range(count):
                nc.tensor.matmul(out=warm_bank[:], lhsT=ones[:, 0:P], rhs=ones[:], start=True, stop=True)

        warm_up(3)
        bias_rows_f32 = consts.tile([P, P], F32, name="bias_rows_f32")
        nc.scalar.copy(out=bias_rows_f32[:], in_=bias_rows[:])
        bias_bank = tp_psum.tile([P, P], F32, name="bias_bank", tag="tp")
        nc.tensor.transpose(out=bias_bank[:], in_=bias_rows_f32[:], identity=ident[:])
        bias_col = consts.tile([P, 2 * UNIT_CHUNKS], F32, name="bias_col")
        nc.scalar.copy(out=bias_col[:], in_=bias_bank[:, 0 : 2 * UNIT_CHUNKS])
        bz_bank = tp_psum.tile([P, FEATURES], F32, name="bz_bank", tag="tp")
        for c in range(UNIT_CHUNKS):
            nc.tensor.matmul(
                out=bz_bank[:, c * P : (c + 1) * P],
                lhsT=ident[:, c : c + 1].to_broadcast([P, P]),
                rhs=bias_rows_f32[:],
                start=True,
                stop=True,
            )
        bz_full = consts.tile([P, FEATURES], F32, name="bz_full")
        nc.scalar.copy(out=bz_full[:], in_=bz_bank[:])
        for pair in range(TILES[0] // 2):
            transpose_operand(0, 0, pair)
        for pair in range(TILES[0] // 2):
            transpose_operand(0, 1, pair)
        grouped_uz = regroup_weight(nc.vector.tensor_copy, raw_uz)
        uz_q = quantise_weight(grouped_uz, "uz")
        grouped_wz = regroup_weight(nc.vector.tensor_copy, raw_wz)
        x0_q = quantise_operand(0, 0)
        wz_q = quantise_weight(grouped_wz, "wz")
        s0_q = quantise_operand(0, 1)
        grouped_ug = regroup_weight(nc.scalar.copy, raw_ug)
        grouped_wg = regroup_weight(nc.vector.tensor_copy, raw_wg)
        operand_q[0] = [x0_q, s0_q]
        weight_q = {GATE_Z: [uz_q, wz_q]}
        last = BLOCKS - 1
        for b in range(1, LOAD_LEAD):
            if b not in x_sb:
                load_x(b)
            if b not in s_sb:
                load_s(b)
            load_h(b - 1)

        for b in range(BLOCKS):
            if b + LOAD_LEAD < BLOCKS:
                load_x(b + LOAD_LEAD)
                load_s(b + LOAD_LEAD)
            if b + LOAD_LEAD - 1 < BLOCKS:
                load_h(b + LOAD_LEAD - 1)
            ahead = b + TRANSPOSE_LEAD
            ahead_pairs = [(side, pair) for side in range(2) for pair in range(TILES[ahead] // 2)] if ahead < BLOCKS else []

            first_pairs = [(side, pair) for side in range(2) for pair in range(TILES[1] // 2)]
            back_first = min(3, TILES[b - 1])
            pre = gate_z_by_rows(b)
            gate_z_by_units(b)
            if b == 0:
                weight_q[GATE_G] = [quantise_weight(grouped_ug, "ug"), quantise_weight(grouped_wg, "wg")]
                for side, pair in first_pairs:
                    transpose_operand(1, side, pair)
            tanh_z_by_rows(b, pre)
            if b > 0:
                for j in range(back_first):
                    g_times_h(b - 1, j)
            gate_g(b, 0)
            if b == 0:
                pass
            else:
                for j in range(back_first, TILES[b - 1]):
                    g_times_h(b - 1, j)
            for j in range(NR[b], TILES[b]):
                z_times_s_by_units(b, j)
            for side, pair in ahead_pairs[:1]:
                transpose_operand(ahead, side, pair)
            if b + 1 < BLOCKS:
                operand_q[b + 1] = [quantise_operand(b + 1, side) for side in range(2)]
            if 0 < b and b - 1 not in EARLY:
                z_times_s_by_rows(b - 1)
            if b in EARLY:
                z_times_s_by_rows(b)
            if b - 1 in GMERGE:
                finish_block(b - 1)
            elif 0 < b:
                for j in range(TILES[b - 1]):
                    if j < GSUBS.get(b - 1, 4):
                        finish(nc.gpsimd, b - 1, j)
            gate_g(b, 1)
            for side, pair in ahead_pairs[1:]:
                transpose_operand(ahead, side, pair)

        for j in range(TILES[last]):
            g_times_h(last, j)
        for j in range(GSUBS.get(last - 1, 4), TILES[last - 1]):
            finish(nc.vector, last - 1, j)
        for j in range(TILES[last]):
            finish(nc.vector, last, j)
